import numpy as np
import ml_dtypes


def mxq(x, axis, fmt="e4m3"):
    dtype, down = {"e4m3": (ml_dtypes.float8_e4m3fn, 7), "e5m2": (ml_dtypes.float8_e5m2, 14)}[fmt]
    v = np.moveaxis(np.asarray(x, np.float32).astype(ml_dtypes.bfloat16).astype(np.float64), axis, -1)
    blocks = v.reshape(v.shape[:-1] + (-1, 32))
    amax = np.abs(blocks).max(-1, keepdims=True)
    byte = np.maximum(np.where(amax > 0, np.frexp(amax)[1] - 1 + 127, 0) - down, 1)
    scale = np.exp2(byte - 127.0)
    codes = (blocks / scale).astype(np.float32).astype(dtype).astype(np.float64)
    return np.moveaxis((codes * scale).reshape(v.shape), -1, axis)


WIDE = False


def mx_kscale(k):
    if not WIDE:
        return np.ones(k)
    levels = np.array([10, -10, 5, -5, 0])
    a = np.random.permutation(np.resize(levels, k // 512 * 4)).reshape(k // 512, 4)
    idx = np.arange(k)
    return np.exp2(a[idx // 512, idx % 128 // 32])


BF16 = ml_dtypes.bfloat16


def bf(x):
    return np.asarray(x, np.float32).astype(BF16)


def f64(x):
    return np.asarray(x).astype(np.float64)


E, T, G, C = 256, 3, 3, 1024
EPS = 1e-5


def silu(v):
    return v / (1.0 + np.exp(-v))


def sigmoid(v):
    return 1.0 / (1.0 + np.exp(-v))


def softplus(v):
    return np.maximum(v, 0.0) + np.log(1.0 + np.exp(-np.abs(v)))


def layer_norm(v, g, b):
    m = v.mean(-1, keepdims=True)
    var = ((v - m) ** 2).mean(-1, keepdims=True)
    return (v - m) / np.sqrt(var + EPS) * g + b


def setup_inputs():
    n = np.random.standard_normal
    s = mx_kscale(C)
    t = mx_kscale(C)
    r = np.sqrt(C)
    return {
        "edge": bf(n((E, C))),
        "h_k": bf(silu(n((E, T, C))) * s),
        "h_m": bf(silu(n((E, T, C))) * s),
        "Wq": bf(n((C, C)) * 0.3 / r),
        "bq": bf(0.2 + n(C) * 0.1),
        "Wk2": bf(n((C, C)) * 0.5 / r / s[:, None]),
        "bk2": bf(0.2 + n(C) * 0.1),
        "Wm2": bf(n((C, C)) * 1.5 / r / s[:, None] * t),
        "bm2": bf(n(C) * 0.2 * t),
        "Wc": bf(n((C, C)) / r / t[:, None]),
        "bc": bf(0.1 + n(C) * 0.1),
        "g_att": bf(1.0 + n(C) * 0.2),
        "b_att": bf(n(C) * 0.2),
        "g_bn": bf(1.0 + n(C) * 0.2),
        "b_bn": bf(n(C) * 0.2),
    }


def reference(edge, h_k, h_m, Wq, bq, Wk2, bk2, Wm2, bm2, Wc, bc, g_att, b_att, g_bn, b_bn):
    x = f64(edge)
    q = (mxq(x, 1, "e4m3") @ mxq(f64(Wq), 0, "e4m3")) + f64(bq)
    k = (mxq(f64(h_k), 2, "e4m3") @ mxq(f64(Wk2), 0, "e4m3")) + f64(bk2)
    msg = (mxq(f64(h_m), 2, "e4m3") @ mxq(f64(Wm2), 0, "e4m3")) + f64(bm2)
    alpha = q[:, None, :] * k / np.sqrt(C)
    gated = msg * sigmoid(layer_norm(alpha, f64(g_att), f64(b_att)))
    out = (mxq(gated, 2, "e4m3") @ mxq(f64(Wc), 0, "e4m3")) + f64(bc)
    out = out.sum(axis=1)
    return softplus(x + layer_norm(out, f64(g_bn), f64(b_bn)))

@@ -1,0 +1,366 @@
+import concourse.mybir as mybir
+from concourse.masks import make_identity
+
+F32 = mybir.dt.float32
+BF16 = mybir.dt.bfloat16
+U32 = mybir.dt.uint32
+U8 = mybir.dt.uint8
+FP8X4 = mybir.dt.float8_e4m3fn_x4
+ALU = mybir.AluOpType
+ACT = mybir.ActivationFunctionType
+
+P = 128
+E = 256
+T = 3
+C = 1024
+A = E // P
+J = C // P
+PACK = 4
+K_PASS = P * PACK
+PASSES = C // K_PASS
+BANK = 512
+HALVES = C // BANK
+EPS = 1e-5
+TINY = 2.0 ** -60
+
+FLOPS = 2 * C * C * (E + 3 * E * T)
+
+BQ, BK, BM, GA, BA = 0, J, 2 * J, 3 * J, 4 * J
+
+
+def half(h):
+    return slice(h * BANK, (h + 1) * BANK)
+
+
+def block(i):
+    return slice(i * P, (i + 1) * P)
+
+
+def tile_comformerconvedgelayer_pb_kernel(
+    tc, edge, h_k, h_m, Wq, bq, Wk2, bk2, Wm2, bm2, Wc, bc, g_att, b_att, g_bn, b_bn, out
+):
+    nc = tc.nc
+    with tc.tile_pool(name="keep", bufs=1) as keep, tc.psum_pool(name="psum", bufs=8) as psum:
+
+        def bank(name):
+            return psum.tile([P, BANK], F32, tag="bank", name=name)
+
+        ident_f32 = keep.tile([P, P], F32)
+        make_identity(nc, ident_f32[:])
+        ident_bf = keep.tile([P, P], BF16)
+        make_identity(nc, ident_bf[:])
+        neg_half = keep.tile([P, 1], F32)
+        nc.vector.memset(neg_half[:], -0.5)
+        tiny = keep.tile([P, 1], F32)
+        nc.vector.memset(tiny[:], TINY)
+        vec_rows = keep.tile([P, P], BF16)
+        nc.vector.memset(vec_rows[:], 0.0)
+        for i, vec in enumerate((bq, bk2, bm2, g_att, b_att)):
+            nc.scalar.dma_start(out=vec_rows[i * J : (i + 1) * J, :], in_=vec.rearrange("(j p) -> j p", p=P))
+        chan = keep.tile([P, 5 * J], F32)
+        warm = keep.tile([P, 1], F32)
+        nc.scalar.activation(out=warm[:], in_=neg_half[:], func=ACT.Sigmoid)
+
+        def chan_col(base, j):
+            return chan[:, base + j : base + j + 1]
+
+        def inverse_root(x):
+            rstd = keep.tile([P, 1], F32, tag="rstd", bufs=4)
+            nc.gpsimd.tensor_tensor(out=rstd[:], in0=x[:], in1=neg_half[:], op=ALU.pow)
+            return rstd
+
+        def mx_group(acc, w_codes, w_scales, j, x_codes, x_scales, rt):
+            for g in range(PASSES):
+                nc.tensor.matmul_mx(
+                    out=acc,
+                    lhsT=w_codes[:, g, block(j)].bitcast(FP8X4),
+                    lhsT_scale=w_scales[:, g, block(j)],
+                    rhs=x_codes[:, rt, block(g)].bitcast(FP8X4),
+                    rhs_scale=x_scales[:, rt, block(g)],
+                    start=(g == 0),
+                    stop=(g == PASSES - 1),
+                )
+
+        edge_raw = keep.tile([P, A, C], BF16)
+        e_codes = keep.tile([P, A, PASSES * P], U32, align_bytes=64)
+        e_scales = keep.tile([P, A, PASSES * P], U8, align_bytes=64)
+        k_codes = keep.tile([P, A * T, PASSES * P], U32, align_bytes=64)
+        k_scales = keep.tile([P, A * T, PASSES * P], U8, align_bytes=64)
+        m_codes = keep.tile([P, A * T, PASSES * P], U32, align_bytes=64)
+        m_scales = keep.tile([P, A * T, PASSES * P], U8, align_bytes=64)
+        g_codes = keep.tile([P, A, PASSES, T * P], U32, align_bytes=64)
+        g_scales = keep.tile([P, A, PASSES, T * P], U8, align_bytes=64)
+        qbT = keep.tile([P, J, E], F32)
+        alphaT = [keep.tile([P, J, T, P], F32, name="alphaT%d" % a) for a in range(A)]
+        sigT = [keep.tile([P, J, T * P], F32, name="sigT%d" % a) for a in range(A)]
+        gated = [keep.tile([P, J, T, P], BF16, name="gated%d" % a) for a in range(A)]
+
+        def key_times_query(a, j, wk):
+            acc = bank("kT")
+            for t in range(T):
+                mx_group(acc[:, block(t)], wk[0], wk[1], j, k_codes, k_scales, a * T + t)
+            nc.vector.scalar_tensor_tensor(
+                out=alphaT[a][:, j, :, :],
+                in0=acc[:, 0 : T * P].rearrange("p (t e) -> p t e", t=T),
+                scalar=chan_col(BK, j),
+                in1=qbT[:, j, block(a)].unsqueeze(1).to_broadcast([P, T, P]),
+                op0=ALU.add,
+                op1=ALU.mult,
+            )
+
+        def normalise_rows(a, t):
+            alpha = [bank("alpha%d" % h) for h in range(HALVES)]
+            for j in range(J):
+                nc.tensor.transpose(alpha[j // PACK][:, block(j % PACK)], alphaT[a][:, j, t, :], ident_f32[:])
+            stats = keep.tile([P, HALVES, 6], F32, tag="stats", bufs=4)
+            for h in range(HALVES):
+                nc.vector.bn_stats(out=stats[:, h, :], in_=alpha[h][:])
+            mean_var = keep.tile([P, 2], F32, tag="mean_var", bufs=4)
+            nc.vector.bn_aggr(out=mean_var[:], in_=stats[:].rearrange("p h s -> p (h s)"))
+            var_eps = keep.tile([P, 1], F32, tag="var_eps", bufs=4)
+            nc.vector.tensor_scalar(out=var_eps[:], in0=mean_var[:, 1:2], scalar1=C * EPS, scalar2=None, op0=ALU.add)
+            rstd = inverse_root(var_eps)
+            shift = keep.tile([P, 1], F32, tag="shift", bufs=4)
+            nc.gpsimd.tensor_scalar(
+                out=shift[:], in0=mean_var[:, 0:1], scalar1=rstd[:], scalar2=-1.0, op0=ALU.mult, op1=ALU.mult
+            )
+            y = keep.tile([P, C], F32, tag="y", bufs=4)
+            for h in range(HALVES):
+                nc.scalar.activation(
+                    out=y[:, half(h)], in_=alpha[h][:], func=ACT.Identity, scale=rstd[:], bias=shift[:]
+                )
+            return y
+
+        def gate_weights(a, j, ys):
+            yT = bank("yT")
+            for t in range(T):
+                nc.tensor.transpose(yT[:, block(t)], ys[t][:, block(j)], ident_f32[:])
+            nc.scalar.activation(
+                out=sigT[a][:, j, :], in_=yT[:, 0 : T * P], func=ACT.Sigmoid,
+                scale=chan_col(GA, j), bias=chan_col(BA, j),
+            )
+
+        def gate_messages(a, j, wm):
+            acc = bank("msgT")
+            for t in range(T):
+                mx_group(acc[:, block(t)], wm[0], wm[1], j, m_codes, m_scales, a * T + t)
+            nc.vector.scalar_tensor_tensor(
+                out=gated[a][:, j, :, :].rearrange("p t e -> p (t e)"),
+                in0=acc[:, 0 : T * P],
+                scalar=chan_col(BM, j),
+                in1=sigT[a][:, j, :],
+                op0=ALU.add,
+                op1=ALU.mult,
+            )
+
+        def quantise_gated(a, g):
+            grouped = keep.tile([P, T * P, PACK], BF16, tag="gated_grouped", bufs=2, align_bytes=64)
+            nc.vector.tensor_copy(
+                out=grouped[:], in_=gated[a][:, g * PACK : (g + 1) * PACK, :, :].rearrange("p f t e -> p (t e) f")
+            )
+            for lo, hi in ((0, 2 * P), (2 * P, 3 * P)):
+                nc.vector.quantize_mx(
+                    out=g_codes[:, a, g, lo:hi].bitcast(FP8X4),
+                    scales=g_scales[:, a, g, lo:hi],
+                    in_=grouped[:, lo:hi, :].rearrange("p r f -> p (r f)"),
+                )
+
+        with tc.tile_pool(name="stage", bufs=1) as stage:
+            def load_rows(x, a):
+                raw = stage.tile([P, T, C], BF16, tag="rows_raw", bufs=3)
+                nc.sync.dma_start(out=raw[:], in_=x[a * P : (a + 1) * P, :, :])
+                return raw
+
+            def load_weight(w, pairs):
+                chunks = []
+                for g in range(PASSES):
+                    raw = stage.tile([P, PACK, C], BF16, tag="w_raw", bufs=4, name="w_raw")
+                    rows = w[g * K_PASS : (g + 1) * K_PASS, :]
+                    if pairs:
+                        nc.sync.dma_start(
+                            out=raw[:].rearrange("p (u e) w -> p u (e w)", u=2),
+                            in_=rows.rearrange("(u p e) w -> p u (e w)", u=2, p=P),
+                        )
+                    else:
+                        nc.sync.dma_start(out=raw[:], in_=rows.rearrange("(f p) w -> p f w", p=P))
+                    chunks.append(raw)
+                return chunks
+
+            nc.sync.dma_start(out=edge_raw[:], in_=edge.rearrange("(a p) c -> p a c", p=P))
+            wq_raw = load_weight(Wq, True)
+            hk_raw = [load_rows(h_k, 0)]
+            wk_raw = load_weight(Wk2, True)
+            hk_raw.append(load_rows(h_k, 1))
+            hm_raw = [load_rows(h_m, a) for a in range(A)]
+            wm_raw = load_weight(Wm2, True)
+            wc_raw = load_weight(Wc, False)
+
+            def quantise_rows(words, codes, scales):
+                wordsT = psum.tile([P, PASSES * 2, P], F32, tag="bank")
+                for s in range(PASSES * 2):
+                    nc.tensor.transpose(wordsT[:, s, :], words[:, block(s)], ident_f32[:])
+                grouped = stage.tile([P, PASSES, P, PACK], BF16, tag="x_grouped", bufs=3, align_bytes=64)
+                nc.scalar.copy(
+                    out=grouped[:].bitcast(F32), in_=wordsT[:].rearrange("p (g u) r -> p g r u", u=2)
+                )
+                nc.vector.quantize_mx(
+                    out=codes.bitcast(FP8X4), scales=scales, in_=grouped[:].rearrange("p g r f -> p (g r f)")
+                )
+
+            def quantise_weight(chunks):
+                codes = keep.tile([P, PASSES, C], U32, tag="w_codes", bufs=3, align_bytes=64)
+                scales = keep.tile([P, PASSES, C], U8, tag="w_scales", bufs=3, align_bytes=64)
+                for g in range(PASSES):
+                    for h in range(HALVES):
+                        grouped = stage.tile([P, BANK, PACK], BF16, tag="w_grouped", bufs=3, align_bytes=64)
+                        dst = grouped[:].rearrange("p (c i) f -> p c f i", i=4)
+                        src = chunks[g][:, :, half(h)].rearrange("p f (c i) -> p c f i", i=4)
+                        if h == 0:
+                            nc.vector.tensor_copy(out=dst, in_=src)
+                        else:
+                            nc.scalar.copy(out=dst, in_=src)
+                        nc.vector.quantize_mx(
+                            out=codes[:, g, half(h)].bitcast(FP8X4),
+                            scales=scales[:, g, half(h)],
+                            in_=grouped[:].rearrange("p w f -> p (w f)"),
+                        )
+                return codes, scales
+
+            def quantise_directions(raw, a, t, codes, scales):
+                quantise_rows(raw[a][:, t, :].bitcast(F32), codes[:, a * T + t, :], scales[:, a * T + t, :])
+
+            for a in range(A):
+                quantise_rows(edge_raw[:, a, :].bitcast(F32), e_codes[:, a, :], e_scales[:, a, :])
+            vec_cols = psum.tile([P, P], BF16, tag="bank")
+            nc.tensor.transpose(vec_cols[:], vec_rows[:], ident_bf[:])
+            nc.vector.tensor_copy(out=chan[:], in_=vec_cols[:, 0 : 5 * J])
+            wq = quantise_weight(wq_raw)
+            for t in range(T):
+                quantise_directions(hk_raw, 0, t, k_codes, k_scales)
+            for j in range(J):
+                acc = bank("qT")
+                for a in range(A):
+                    mx_group(acc[:, block(a)], wq[0], wq[1], j, e_codes, e_scales, a)
+                nc.scalar.activation(
+                    out=qbT[:, j, :], in_=acc[:, 0:E], func=ACT.Identity, bias=chan_col(BQ, j), scale=1.0
+                )
+            wk = quantise_weight(wk_raw)
+            for t in range(T):
+                quantise_directions(hk_raw, 1, t, k_codes, k_scales)
+
+            for j in range(J):
+                key_times_query(0, j, wk)
+            for j in range(2):
+                key_times_query(1, j, wk)
+            ys = [[], []]
+            for t in range(T):
+                ys[0].append(normalise_rows(0, t))
+                for j in (2 + 2 * t, 3 + 2 * t):
+                    key_times_query(1, j, wk)
+                quantise_directions(hm_raw, 0, t, m_codes, m_scales)
+            wm = quantise_weight(wm_raw)
+            for t in range(T):
+                quantise_directions(hm_raw, 1, t, m_codes, m_scales)
+            for t in range(T):
+                ys[1].append(normalise_rows(1, t))
+            for j in range(J):
+                gate_weights(0, j, ys[0])
+            for j in range(J):
+                gate_messages(0, j, wm)
+                if j % PACK == PACK - 1:
+                    quantise_gated(0, j // PACK)
+            wc = quantise_weight(wc_raw)
+
+        with tc.tile_pool(name="late", bufs=1, reuse_waits="tile") as late:
+            bc_all = late.tile([P, C], BF16)
+            nc.sync.dma_start(out=bc_all[:], in_=bc.partition_broadcast(P))
+            g_all = late.tile([P, C], BF16)
+            nc.sync.dma_start(out=g_all[:], in_=g_bn.partition_broadcast(P))
+            b_all = late.tile([P, C], BF16)
+            nc.sync.dma_start(out=b_all[:], in_=b_bn.partition_broadcast(P))
+            edge_b = late.tile([P, A, C], F32)
+            for a in range(A):
+                nc.gpsimd.tensor_tensor(out=edge_b[:, a, :], in0=edge_raw[:, a, :], in1=b_all[:], op=ALU.add)
+
+            u_acc = {}
+
+            def sum_directions(a, g):
+                if g == 0:
+                    u_acc[a] = [bank("u%d" % h) for h in range(HALVES)]
+                for t in range(T):
+                    for h in range(HALVES):
+                        nc.tensor.matmul_mx(
+                            out=u_acc[a][h][:],
+                            lhsT=g_codes[:, a, g, block(t)].bitcast(FP8X4),
+                            lhsT_scale=g_scales[:, a, g, block(t)],
+                            rhs=wc[0][:, g, half(h)].bitcast(FP8X4),
+                            rhs_scale=wc[1][:, g, half(h)],
+                            start=(g == 0 and t == 0),
+                            stop=(g == PASSES - 1 and t == T - 1),
+                        )
+
+            for j in range(J):
+                gate_weights(1, j, ys[1])
+            for g in range(PASSES):
+                sum_directions(0, g)
+            for j in range(J):
+                gate_messages(1, j, wm)
+                if j % PACK == PACK - 1:
+                    quantise_gated(1, j // PACK)
+                    sum_directions(1, j // PACK)
+
+            vs = []
+            logs = []
+            for a in range(A):
+                ub = late.tile([P, C], F32, tag="ub", bufs=2)
+                sums = late.tile([P, HALVES], F32, tag="sums", bufs=2)
+                for h in range(HALVES):
+                    nc.vector.scalar_tensor_tensor(
+                        out=ub[:, half(h)], in0=bc_all[:, half(h)], scalar=float(T), in1=u_acc[a][h][:],
+                        op0=ALU.mult, op1=ALU.add, accum_out=sums[:, h : h + 1],
+                    )
+                neg_mean = late.tile([P, 1], F32, tag="neg_mean", bufs=2)
+                nc.vector.tensor_scalar(
+                    out=neg_mean[:], in0=sums[:, 0:1], scalar1=sums[:, 1:2], scalar2=-1.0 / C,
+                    op0=ALU.add, op1=ALU.mult,
+                )
+                neg_mean_root = late.tile([P, 1], F32, tag="neg_mean_root", bufs=2)
+                nc.vector.tensor_scalar(
+                    out=neg_mean_root[:], in0=sums[:, 0:1], scalar1=sums[:, 1:2], scalar2=-1.0 / (C * C ** 0.5),
+                    op0=ALU.add, op1=ALU.mult,
+                )
+                squares = late.tile([P, C], F32, tag="squares", bufs=1)
+                var = late.tile([P, HALVES], F32, tag="var", bufs=2)
+                for h in range(HALVES):
+                    nc.scalar.activation(
+                        out=squares[:, half(h)], in_=ub[:, half(h)], func=ACT.Square,
+                        scale=C ** -0.5, bias=neg_mean_root[:], accum_out=var[:, h : h + 1],
+                    )
+                v = late.tile([P, C], F32, tag="v", bufs=2)
+                for h in range(HALVES):
+                    nc.vector.scalar_tensor_tensor(
+                        out=v[:, half(h)], in0=ub[:, half(h)], scalar=neg_mean[:], in1=g_all[:, half(h)],
+                        op0=ALU.add, op1=ALU.mult,
+                    )
+                var_eps = late.tile([P, 1], F32, tag="var_eps_out", bufs=2)
+                nc.vector.tensor_scalar(
+                    out=var_eps[:], in0=var[:, 0:1], scalar1=var[:, 1:2], scalar2=EPS, op0=ALU.add, op1=ALU.add
+                )
+                rstd = inverse_root(var_eps)
+                log = late.tile([P, C], F32, tag="log", bufs=2)
+                for h in range(HALVES):
+                    nc.vector.scalar_tensor_tensor(
+                        out=v[:, half(h)], in0=v[:, half(h)], scalar=rstd[:], in1=edge_b[:, a, half(h)],
+                        op0=ALU.mult, op1=ALU.add,
+                    )
+                    nc.scalar.activation(out=log[:, half(h)], in_=v[:, half(h)], func=ACT.Sigmoid, scale=-1.0)
+                vs.append(v)
+                logs.append(log)
+            for a in range(A):
+                for h in range(HALVES):
+                    nc.scalar.activation(out=logs[a][:, half(h)], in_=logs[a][:, half(h)], func=ACT.Ln, bias=tiny[:])
+                    nc.vector.scalar_tensor_tensor(
+                        out=logs[a][:, half(h)], in0=logs[a][:, half(h)], scalar=-1.0, in1=vs[a][:, half(h)],
+                        op0=ALU.mult, op1=ALU.max,
+                    )
+                    nc.sync.dma_start(out=out[a * P : (a + 1) * P, half(h)], in_=logs[a][:, half(h)])

@@ -40,7 +40,7 @@ def tile_comformerconvedgelayer_pb_kernel(
     tc, edge, h_k, h_m, Wq, bq, Wk2, bk2, Wm2, bm2, Wc, bc, g_att, b_att, g_bn, b_bn, out
 ):
     nc = tc.nc
-    with tc.tile_pool(name="keep", bufs=1) as keep, tc.psum_pool(name="psum", bufs=8) as psum:
+    with tc.tile_pool(name="keep", bufs=1) as keep, tc.psum_pool(name="psum", bufs=8) as psum, tc.manual_schedule():
 
         def bank(name):
             return psum.tile([P, BANK], F32, tag="bank", name=name)
@@ -64,303 +64,414 @@ def tile_comformerconvedgelayer_pb_kernel(
         def chan_col(base, j):
             return chan[:, base + j : base + j + 1]
 
-        def inverse_root(x):
-            rstd = keep.tile([P, 1], F32, tag="rstd", bufs=4)
-            nc.gpsimd.tensor_tensor(out=rstd[:], in0=x[:], in1=neg_half[:], op=ALU.pow)
-            return rstd
+        edge_raw = keep.tile([P, A, C], BF16)
+        x_codes = {}
+        x_scales = {}
+        for name, row_tiles in (("e", A), ("k", A * T), ("m", A * T)):
+            x_codes[name] = keep.tile([P, row_tiles, PASSES * P], U32, name="codes_" + name, align_bytes=64)
+            x_scales[name] = keep.tile([P, row_tiles, PASSES * P], U8, name="scales_" + name, align_bytes=64)
+        g_codes = keep.tile([P, A, PASSES, T * P], U32, align_bytes=64)
+        g_scales = keep.tile([P, A, PASSES, T * P], U8, align_bytes=64)
+        w_codes = {}
+        w_scales = {}
+        qbT = keep.tile([P, J, E], F32, tag="qbT_then_edge_b")
+        alphaT = [keep.tile([P, J, T, P], F32, name="alphaT%d" % a) for a in range(A)]
+        sigT = [keep.tile([P, J, T * P], F32, name="sigT%d" % a) for a in range(A)]
+        gated = [keep.tile([P, J, T, P], BF16, name="gated%d" % a) for a in range(A)]
+        bc_all = keep.tile([P, C], BF16)
+        g_all = keep.tile([P, C], BF16)
+        b_all = keep.tile([P, C], BF16)
+        acc = {}
+        grouped = {}
+        stats = {}
+        rstd = {}
+        shift = {}
+        mean_var = {}
+        ys = {}
 
-        def mx_group(acc, w_codes, w_scales, j, x_codes, x_scales, rt):
+        def new_weight(name):
+            w_codes[name] = keep.tile([P, PASSES, C], U32, tag="w_codes", bufs=3, name="codes_" + name, align_bytes=64)
+            w_scales[name] = keep.tile([P, PASSES, C], U8, tag="w_scales", bufs=3, name="scales_" + name, align_bytes=64)
+
+        def mx_group(out_cols, w, j, x, rt):
             for g in range(PASSES):
                 nc.tensor.matmul_mx(
-                    out=acc,
-                    lhsT=w_codes[:, g, block(j)].bitcast(FP8X4),
-                    lhsT_scale=w_scales[:, g, block(j)],
-                    rhs=x_codes[:, rt, block(g)].bitcast(FP8X4),
-                    rhs_scale=x_scales[:, rt, block(g)],
+                    out=out_cols,
+                    lhsT=w_codes[w][:, g, block(j)].bitcast(FP8X4),
+                    lhsT_scale=w_scales[w][:, g, block(j)],
+                    rhs=x_codes[x][:, rt, block(g)].bitcast(FP8X4),
+                    rhs_scale=x_scales[x][:, rt, block(g)],
                     start=(g == 0),
                     stop=(g == PASSES - 1),
                 )
 
-        edge_raw = keep.tile([P, A, C], BF16)
-        e_codes = keep.tile([P, A, PASSES * P], U32, align_bytes=64)
-        e_scales = keep.tile([P, A, PASSES * P], U8, align_bytes=64)
-        k_codes = keep.tile([P, A * T, PASSES * P], U32, align_bytes=64)
-        k_scales = keep.tile([P, A * T, PASSES * P], U8, align_bytes=64)
-        m_codes = keep.tile([P, A * T, PASSES * P], U32, align_bytes=64)
-        m_scales = keep.tile([P, A * T, PASSES * P], U8, align_bytes=64)
-        g_codes = keep.tile([P, A, PASSES, T * P], U32, align_bytes=64)
-        g_scales = keep.tile([P, A, PASSES, T * P], U8, align_bytes=64)
-        qbT = keep.tile([P, J, E], F32)
-        alphaT = [keep.tile([P, J, T, P], F32, name="alphaT%d" % a) for a in range(A)]
-        sigT = [keep.tile([P, J, T * P], F32, name="sigT%d" % a) for a in range(A)]
-        gated = [keep.tile([P, J, T, P], BF16, name="gated%d" % a) for a in range(A)]
+        def inverse_std(key, eps):
+            var_eps = keep.tile([P, 1], F32, tag="var_eps", bufs=4)
+            nc.gpsimd.tensor_scalar(
+                out=var_eps[:], in0=mean_var[key][:, 1:2], scalar1=eps, scalar2=1.0, op0=ALU.add, op1=ALU.mult
+            )
+            rstd[key] = keep.tile([P, 1], F32, tag="rstd", bufs=4, name="rstd")
+            nc.gpsimd.tensor_tensor(out=rstd[key][:], in0=var_eps[:], in1=neg_half[:], op=ALU.pow)
 
-        def key_times_query(a, j, wk):
-            acc = bank("kT")
+        def aggregate(key):
+            mean_var[key] = keep.tile([P, 2], F32, tag="mean_var", bufs=4, name="mean_var")
+            nc.vector.bn_aggr(out=mean_var[key][:], in_=stats[key][:].rearrange("p h s -> p (h s)"))
+
+        def query_products(j):
+            acc["q", j] = bank("qT")
+            for a in range(A):
+                mx_group(acc["q", j][:, block(a)], "q", j, "e", a)
+
+        def add_query_bias(j):
+            nc.scalar.activation(
+                out=qbT[:, j, :], in_=acc["q", j][:, 0:E], func=ACT.Identity, bias=chan_col(BQ, j), scale=1.0
+            )
+
+        def key_products(a, j):
+            acc["k", a, j] = bank("kT")
             for t in range(T):
-                mx_group(acc[:, block(t)], wk[0], wk[1], j, k_codes, k_scales, a * T + t)
+                mx_group(acc["k", a, j][:, block(t)], "k", j, "k", a * T + t)
+
+        def times_query(a, j):
             nc.vector.scalar_tensor_tensor(
                 out=alphaT[a][:, j, :, :],
-                in0=acc[:, 0 : T * P].rearrange("p (t e) -> p t e", t=T),
+                in0=acc["k", a, j][:, 0 : T * P].rearrange("p (t e) -> p t e", t=T),
                 scalar=chan_col(BK, j),
                 in1=qbT[:, j, block(a)].unsqueeze(1).to_broadcast([P, T, P]),
                 op0=ALU.add,
                 op1=ALU.mult,
             )
 
-        def normalise_rows(a, t):
-            alpha = [bank("alpha%d" % h) for h in range(HALVES)]
+        def transpose_alpha(a, t):
+            acc["alpha", a, t] = [bank("alpha%d" % h) for h in range(HALVES)]
             for j in range(J):
-                nc.tensor.transpose(alpha[j // PACK][:, block(j % PACK)], alphaT[a][:, j, t, :], ident_f32[:])
-            stats = keep.tile([P, HALVES, 6], F32, tag="stats", bufs=4)
+                nc.tensor.transpose(
+                    acc["alpha", a, t][j // PACK][:, block(j % PACK)], alphaT[a][:, j, t, :], ident_f32[:]
+                )
+
+        def row_stats(a, t):
+            stats[a, t] = keep.tile([P, HALVES, 6], F32, tag="stats", bufs=4, name="stats")
             for h in range(HALVES):
-                nc.vector.bn_stats(out=stats[:, h, :], in_=alpha[h][:])
-            mean_var = keep.tile([P, 2], F32, tag="mean_var", bufs=4)
-            nc.vector.bn_aggr(out=mean_var[:], in_=stats[:].rearrange("p h s -> p (h s)"))
-            var_eps = keep.tile([P, 1], F32, tag="var_eps", bufs=4)
-            nc.vector.tensor_scalar(out=var_eps[:], in0=mean_var[:, 1:2], scalar1=C * EPS, scalar2=None, op0=ALU.add)
-            rstd = inverse_root(var_eps)
-            shift = keep.tile([P, 1], F32, tag="shift", bufs=4)
+                nc.vector.bn_stats(out=stats[a, t][:, h, :], in_=acc["alpha", a, t][h][:])
+
+        def row_scale(a, t):
+            aggregate((a, t))
+            inverse_std((a, t), C * EPS)
+            shift[a, t] = keep.tile([P, 1], F32, tag="shift", bufs=4, name="shift")
             nc.gpsimd.tensor_scalar(
-                out=shift[:], in0=mean_var[:, 0:1], scalar1=rstd[:], scalar2=-1.0, op0=ALU.mult, op1=ALU.mult
+                out=shift[a, t][:], in0=mean_var[a, t][:, 0:1], scalar1=rstd[a, t][:], scalar2=-1.0,
+                op0=ALU.mult, op1=ALU.mult,
             )
-            y = keep.tile([P, C], F32, tag="y", bufs=4)
+
+        def normalise(a, t):
+            ys[a, t] = keep.tile([P, C], F32, tag="y", bufs=4, name="y")
             for h in range(HALVES):
                 nc.scalar.activation(
-                    out=y[:, half(h)], in_=alpha[h][:], func=ACT.Identity, scale=rstd[:], bias=shift[:]
+                    out=ys[a, t][:, half(h)], in_=acc["alpha", a, t][h][:], func=ACT.Identity,
+                    scale=rstd[a, t][:], bias=shift[a, t][:],
                 )
-            return y
 
-        def gate_weights(a, j, ys):
+        def gate_weights(a, j):
             yT = bank("yT")
             for t in range(T):
-                nc.tensor.transpose(yT[:, block(t)], ys[t][:, block(j)], ident_f32[:])
+                nc.tensor.transpose(yT[:, block(t)], ys[a, t][:, block(j)], ident_f32[:])
             nc.scalar.activation(
                 out=sigT[a][:, j, :], in_=yT[:, 0 : T * P], func=ACT.Sigmoid,
                 scale=chan_col(GA, j), bias=chan_col(BA, j),
             )
 
-        def gate_messages(a, j, wm):
-            acc = bank("msgT")
+        def gate_messages(a, j):
+            msgT = bank("msgT")
             for t in range(T):
-                mx_group(acc[:, block(t)], wm[0], wm[1], j, m_codes, m_scales, a * T + t)
+                mx_group(msgT[:, block(t)], "m", j, "m", a * T + t)
             nc.vector.scalar_tensor_tensor(
                 out=gated[a][:, j, :, :].rearrange("p t e -> p (t e)"),
-                in0=acc[:, 0 : T * P],
+                in0=msgT[:, 0 : T * P],
                 scalar=chan_col(BM, j),
                 in1=sigT[a][:, j, :],
                 op0=ALU.add,
                 op1=ALU.mult,
             )
 
-        def quantise_gated(a, g):
-            grouped = keep.tile([P, T * P, PACK], BF16, tag="gated_grouped", bufs=2, align_bytes=64)
-            nc.vector.tensor_copy(
-                out=grouped[:], in_=gated[a][:, g * PACK : (g + 1) * PACK, :, :].rearrange("p f t e -> p (t e) f")
+        def regroup_gated(a, g):
+            grouped["g", a, g] = keep.tile(
+                [P, T * P, PACK], BF16, tag="gated_grouped", bufs=2, name="gated_grouped", align_bytes=64
             )
+            nc.vector.tensor_copy(
+                out=grouped["g", a, g][:],
+                in_=gated[a][:, g * PACK : (g + 1) * PACK, :, :].rearrange("p f t e -> p (t e) f"),
+            )
+
+        def quantise_gated(a, g):
             for lo, hi in ((0, 2 * P), (2 * P, 3 * P)):
                 nc.vector.quantize_mx(
                     out=g_codes[:, a, g, lo:hi].bitcast(FP8X4),
                     scales=g_scales[:, a, g, lo:hi],
-                    in_=grouped[:, lo:hi, :].rearrange("p r f -> p (r f)"),
+                    in_=grouped["g", a, g][:, lo:hi, :].rearrange("p r f -> p (r f)"),
                 )
 
-        with tc.tile_pool(name="stage", bufs=1) as stage:
-            def load_rows(x, a):
-                raw = stage.tile([P, T, C], BF16, tag="rows_raw", bufs=3)
-                nc.sync.dma_start(out=raw[:], in_=x[a * P : (a + 1) * P, :, :])
-                return raw
+        def gate_edge_tile(a):
+            for j in range(J):
+                gate_messages(a, j)
+                if j == PACK:
+                    regroup_gated(a, 0)
+                if j == PACK + 2:
+                    quantise_gated(a, 0)
 
-            def load_weight(w, pairs):
-                chunks = []
+        with tc.tile_pool(name="stage", bufs=1) as stage:
+            rows_raw = {}
+            w_raw = {}
+
+            def load_rows(name, x, a):
+                rows_raw[name, a] = stage.tile([P, T, C], BF16, tag="rows_raw", bufs=3, name="rows_raw")
+                nc.sync.dma_start(out=rows_raw[name, a][:], in_=x[a * P : (a + 1) * P, :, :])
+
+            def load_weight(name, w, pairs):
                 for g in range(PASSES):
-                    raw = stage.tile([P, PACK, C], BF16, tag="w_raw", bufs=4, name="w_raw")
+                    w_raw[name, g] = stage.tile([P, PACK, C], BF16, tag="w_raw", bufs=4, name="w_raw")
                     rows = w[g * K_PASS : (g + 1) * K_PASS, :]
                     if pairs:
                         nc.sync.dma_start(
-                            out=raw[:].rearrange("p (u e) w -> p u (e w)", u=2),
+                            out=w_raw[name, g][:].rearrange("p (u e) w -> p u (e w)", u=2),
                             in_=rows.rearrange("(u p e) w -> p u (e w)", u=2, p=P),
                         )
                     else:
-                        nc.sync.dma_start(out=raw[:], in_=rows.rearrange("(f p) w -> p f w", p=P))
-                    chunks.append(raw)
-                return chunks
+                        nc.sync.dma_start(out=w_raw[name, g][:], in_=rows.rearrange("(f p) w -> p f w", p=P))
 
             nc.sync.dma_start(out=edge_raw[:], in_=edge.rearrange("(a p) c -> p a c", p=P))
-            wq_raw = load_weight(Wq, True)
-            hk_raw = [load_rows(h_k, 0)]
-            wk_raw = load_weight(Wk2, True)
-            hk_raw.append(load_rows(h_k, 1))
-            hm_raw = [load_rows(h_m, a) for a in range(A)]
-            wm_raw = load_weight(Wm2, True)
-            wc_raw = load_weight(Wc, False)
+            load_weight("q", Wq, True)
+            load_rows("k", h_k, 0)
+            load_weight("k", Wk2, True)
+            load_rows("k", h_k, 1)
+            load_rows("m", h_m, 0)
+            load_rows("m", h_m, 1)
+            load_weight("m", Wm2, True)
+            load_weight("c", Wc, False)
+            nc.sync.dma_start(out=b_all[:], in_=b_bn.partition_broadcast(P))
+            nc.sync.dma_start(out=bc_all[:], in_=bc.partition_broadcast(P))
+            nc.sync.dma_start(out=g_all[:], in_=g_bn.partition_broadcast(P))
 
-            def quantise_rows(words, codes, scales):
+            def rows_to_words(name, rt, words):
                 wordsT = psum.tile([P, PASSES * 2, P], F32, tag="bank")
                 for s in range(PASSES * 2):
                     nc.tensor.transpose(wordsT[:, s, :], words[:, block(s)], ident_f32[:])
-                grouped = stage.tile([P, PASSES, P, PACK], BF16, tag="x_grouped", bufs=3, align_bytes=64)
+                grouped[name, rt] = stage.tile(
+                    [P, PASSES, P, PACK], BF16, tag="x_grouped", bufs=3, name="x_grouped", align_bytes=64
+                )
                 nc.scalar.copy(
-                    out=grouped[:].bitcast(F32), in_=wordsT[:].rearrange("p (g u) r -> p g r u", u=2)
+                    out=grouped[name, rt][:].bitcast(F32), in_=wordsT[:].rearrange("p (g u) r -> p g r u", u=2)
                 )
+
+            def quantise_rows(name, rt):
                 nc.vector.quantize_mx(
-                    out=codes.bitcast(FP8X4), scales=scales, in_=grouped[:].rearrange("p g r f -> p (g r f)")
+                    out=x_codes[name][:, rt, :].bitcast(FP8X4),
+                    scales=x_scales[name][:, rt, :],
+                    in_=grouped[name, rt][:].rearrange("p g r f -> p (g r f)"),
                 )
 
-            def quantise_weight(chunks):
-                codes = keep.tile([P, PASSES, C], U32, tag="w_codes", bufs=3, align_bytes=64)
-                scales = keep.tile([P, PASSES, C], U8, tag="w_scales", bufs=3, align_bytes=64)
-                for g in range(PASSES):
-                    for h in range(HALVES):
-                        grouped = stage.tile([P, BANK, PACK], BF16, tag="w_grouped", bufs=3, align_bytes=64)
-                        dst = grouped[:].rearrange("p (c i) f -> p c f i", i=4)
-                        src = chunks[g][:, :, half(h)].rearrange("p f (c i) -> p c f i", i=4)
-                        if h == 0:
-                            nc.vector.tensor_copy(out=dst, in_=src)
-                        else:
-                            nc.scalar.copy(out=dst, in_=src)
-                        nc.vector.quantize_mx(
-                            out=codes[:, g, half(h)].bitcast(FP8X4),
-                            scales=scales[:, g, half(h)],
-                            in_=grouped[:].rearrange("p w f -> p (w f)"),
-                        )
-                return codes, scales
+            def directions_to_words(name, a):
+                for t in range(T):
+                    rows_to_words(name, a * T + t, rows_raw[name, a][:, t, :].bitcast(F32))
 
-            def quantise_directions(raw, a, t, codes, scales):
-                quantise_rows(raw[a][:, t, :].bitcast(F32), codes[:, a * T + t, :], scales[:, a * T + t, :])
+            def quantise_directions(name, a):
+                for t in range(T):
+                    quantise_rows(name, a * T + t)
+
+            def regroup(name, g, h, on_scalar):
+                grouped[name, g, h] = stage.tile(
+                    [P, BANK, PACK], BF16, tag="w_grouped", bufs=4, name="w_grouped", align_bytes=64
+                )
+                dst = grouped[name, g, h][:].rearrange("p (c i) f -> p c f i", i=4)
+                src = w_raw[name, g][:, :, half(h)].rearrange("p f (c i) -> p c f i", i=4)
+                if on_scalar:
+                    nc.scalar.copy(out=dst, in_=src)
+                else:
+                    nc.vector.tensor_copy(out=dst, in_=src)
+
+            def quantise_piece(name, g, h):
+                nc.vector.quantize_mx(
+                    out=w_codes[name][:, g, half(h)].bitcast(FP8X4),
+                    scales=w_scales[name][:, g, half(h)],
+                    in_=grouped[name, g, h][:].rearrange("p w f -> p (w f)"),
+                )
 
             for a in range(A):
-                quantise_rows(edge_raw[:, a, :].bitcast(F32), e_codes[:, a, :], e_scales[:, a, :])
+                rows_to_words("e", a, edge_raw[:, a, :].bitcast(F32))
             vec_cols = psum.tile([P, P], BF16, tag="bank")
             nc.tensor.transpose(vec_cols[:], vec_rows[:], ident_bf[:])
+            for a in range(A):
+                quantise_rows("e", a)
             nc.vector.tensor_copy(out=chan[:], in_=vec_cols[:, 0 : 5 * J])
-            wq = quantise_weight(wq_raw)
-            for t in range(T):
-                quantise_directions(hk_raw, 0, t, k_codes, k_scales)
+            new_weight("q")
+            for g in range(PASSES):
+                regroup("q", g, 0, False)
+                regroup("q", g, 1, True)
+            for g in range(PASSES):
+                for h in range(HALVES):
+                    quantise_piece("q", g, h)
+            directions_to_words("k", 0)
             for j in range(J):
-                acc = bank("qT")
-                for a in range(A):
-                    mx_group(acc[:, block(a)], wq[0], wq[1], j, e_codes, e_scales, a)
-                nc.scalar.activation(
-                    out=qbT[:, j, :], in_=acc[:, 0:E], func=ACT.Identity, bias=chan_col(BQ, j), scale=1.0
-                )
-            wk = quantise_weight(wk_raw)
-            for t in range(T):
-                quantise_directions(hk_raw, 1, t, k_codes, k_scales)
+                query_products(j)
 
+            new_weight("k")
+            regroup("k", 0, 0, False)
+            regroup("k", 0, 1, True)
+            quantise_directions("k", 0)
             for j in range(J):
-                key_times_query(0, j, wk)
+                add_query_bias(j)
+            regroup("k", 1, 0, False)
+            quantise_piece("k", 0, 0)
+            regroup("k", 1, 1, False)
+            quantise_piece("k", 0, 1)
+            quantise_piece("k", 1, 0)
+            directions_to_words("k", 1)
+            directions_to_words("m", 0)
+            for j in range(J // 2):
+                key_products(0, j)
+            quantise_piece("k", 1, 1)
+            quantise_directions("k", 1)
+            for j in range(J // 2, J):
+                key_products(0, j)
+
+            new_weight("m")
+            regroup("m", 0, 0, True)
+            for j in range(J):
+                times_query(0, j)
             for j in range(2):
-                key_times_query(1, j, wk)
-            ys = [[], []]
-            for t in range(T):
-                ys[0].append(normalise_rows(0, t))
-                for j in (2 + 2 * t, 3 + 2 * t):
-                    key_times_query(1, j, wk)
-                quantise_directions(hm_raw, 0, t, m_codes, m_scales)
-            wm = quantise_weight(wm_raw)
-            for t in range(T):
-                quantise_directions(hm_raw, 1, t, m_codes, m_scales)
-            for t in range(T):
-                ys[1].append(normalise_rows(1, t))
-            for j in range(J):
-                gate_weights(0, j, ys[0])
-            for j in range(J):
-                gate_messages(0, j, wm)
-                if j % PACK == PACK - 1:
-                    quantise_gated(0, j // PACK)
-            wc = quantise_weight(wc_raw)
+                key_products(1, j)
 
-        with tc.tile_pool(name="late", bufs=1, reuse_waits="tile") as late:
-            bc_all = late.tile([P, C], BF16)
-            nc.sync.dma_start(out=bc_all[:], in_=bc.partition_broadcast(P))
-            g_all = late.tile([P, C], BF16)
-            nc.sync.dma_start(out=g_all[:], in_=g_bn.partition_broadcast(P))
-            b_all = late.tile([P, C], BF16)
-            nc.sync.dma_start(out=b_all[:], in_=b_bn.partition_broadcast(P))
-            edge_b = late.tile([P, A, C], F32)
+            for t in range(T):
+                transpose_alpha(0, t)
+                for j in (2 * t + 2, 2 * t + 3):
+                    key_products(1, j)
+                for j in (2 * t, 2 * t + 1):
+                    times_query(1, j)
+                row_stats(0, t)
+                if t == 0:
+                    quantise_directions("m", 0)
+                else:
+                    quantise_piece("m", 0, t - 1)
+                row_scale(0, t)
+                if t == 0:
+                    directions_to_words("m", 1)
+                else:
+                    regroup("m", t - 1, 1, True)
+                normalise(0, t)
+            for j in (J - 2, J - 1):
+                times_query(1, j)
+
+            transpose_alpha(1, 0)
+            transpose_alpha(1, 1)
+            quantise_directions("m", 1)
+            regroup("m", 1, 0, False)
+            new_weight("c")
+            for t in range(T):
+                row_stats(1, t)
+                if t < 2:
+                    quantise_piece("m", 1, t)
+                else:
+                    regroup("c", 0, 0, False)
+                row_scale(1, t)
+                if t == 0:
+                    for j in range(J):
+                        gate_weights(0, j)
+                    transpose_alpha(1, 2)
+                else:
+                    normalise(1, t - 1)
+            normalise(1, T - 1)
+
+            edge_b = keep.tile([P, A, C], F32, tag="qbT_then_edge_b")
             for a in range(A):
                 nc.gpsimd.tensor_tensor(out=edge_b[:, a, :], in0=edge_raw[:, a, :], in1=b_all[:], op=ALU.add)
 
-            u_acc = {}
+            regroup("c", 0, 1, True)
+            quantise_piece("c", 0, 0)
+            gate_edge_tile(0)
+            regroup_gated(0, 1)
+            for j in range(J):
+                gate_weights(1, j)
+            regroup("c", 1, 0, True)
+            regroup("c", 1, 1, True)
+            quantise_piece("c", 0, 1)
+            quantise_gated(0, 1)
+            gate_edge_tile(1)
+            quantise_piece("c", 1, 0)
+            regroup_gated(1, 1)
+            quantise_piece("c", 1, 1)
+
+        with tc.tile_pool(name="late", bufs=1, reuse_waits="tile") as late:
 
             def sum_directions(a, g):
                 if g == 0:
-                    u_acc[a] = [bank("u%d" % h) for h in range(HALVES)]
+                    acc["u", a] = [bank("u%d" % h) for h in range(HALVES)]
                 for t in range(T):
                     for h in range(HALVES):
                         nc.tensor.matmul_mx(
-                            out=u_acc[a][h][:],
+                            out=acc["u", a][h][:],
                             lhsT=g_codes[:, a, g, block(t)].bitcast(FP8X4),
                             lhsT_scale=g_scales[:, a, g, block(t)],
-                            rhs=wc[0][:, g, half(h)].bitcast(FP8X4),
-                            rhs_scale=wc[1][:, g, half(h)],
+                            rhs=w_codes["c"][:, g, half(h)].bitcast(FP8X4),
+                            rhs_scale=w_scales["c"][:, g, half(h)],
                             start=(g == 0 and t == 0),
                             stop=(g == PASSES - 1 and t == T - 1),
                         )
 
-            for j in range(J):
-                gate_weights(1, j, ys[1])
-            for g in range(PASSES):
-                sum_directions(0, g)
-            for j in range(J):
-                gate_messages(1, j, wm)
-                if j % PACK == PACK - 1:
-                    quantise_gated(1, j // PACK)
-                    sum_directions(1, j // PACK)
+            v = [late.tile([P, C], F32, name="v%d" % a) for a in range(A)]
+            log = [late.tile([P, C], F32, name="log%d" % a) for a in range(A)]
 
-            vs = []
-            logs = []
-            for a in range(A):
-                ub = late.tile([P, C], F32, tag="ub", bufs=2)
-                sums = late.tile([P, HALVES], F32, tag="sums", bufs=2)
-                for h in range(HALVES):
-                    nc.vector.scalar_tensor_tensor(
-                        out=ub[:, half(h)], in0=bc_all[:, half(h)], scalar=float(T), in1=u_acc[a][h][:],
-                        op0=ALU.mult, op1=ALU.add, accum_out=sums[:, h : h + 1],
-                    )
-                neg_mean = late.tile([P, 1], F32, tag="neg_mean", bufs=2)
-                nc.vector.tensor_scalar(
-                    out=neg_mean[:], in0=sums[:, 0:1], scalar1=sums[:, 1:2], scalar2=-1.0 / C,
-                    op0=ALU.add, op1=ALU.mult,
+            def add_bias(a, h):
+                nc.vector.scalar_tensor_tensor(
+                    out=v[a][:, half(h)], in0=bc_all[:, half(h)], scalar=float(T), in1=acc["u", a][h][:],
+                    op0=ALU.mult, op1=ALU.add,
                 )
-                neg_mean_root = late.tile([P, 1], F32, tag="neg_mean_root", bufs=2)
-                nc.vector.tensor_scalar(
-                    out=neg_mean_root[:], in0=sums[:, 0:1], scalar1=sums[:, 1:2], scalar2=-1.0 / (C * C ** 0.5),
-                    op0=ALU.add, op1=ALU.mult,
+
+            def out_stats(a):
+                stats["out", a] = keep.tile([P, HALVES, 6], F32, tag="stats", bufs=4, name="stats")
+                for h in range(HALVES):
+                    nc.vector.bn_stats(out=stats["out", a][:, h, :], in_=v[a][:, half(h)])
+
+            def out_scale(a):
+                aggregate(("out", a))
+                inverse_std(("out", a), EPS)
+
+            def centre_times_gain(a, h):
+                nc.vector.scalar_tensor_tensor(
+                    out=v[a][:, half(h)], in0=v[a][:, half(h)], scalar=mean_var["out", a][:, 0:1],
+                    in1=g_all[:, half(h)], op0=ALU.subtract, op1=ALU.mult,
                 )
-                squares = late.tile([P, C], F32, tag="squares", bufs=1)
-                var = late.tile([P, HALVES], F32, tag="var", bufs=2)
-                for h in range(HALVES):
-                    nc.scalar.activation(
-                        out=squares[:, half(h)], in_=ub[:, half(h)], func=ACT.Square,
-                        scale=C ** -0.5, bias=neg_mean_root[:], accum_out=var[:, h : h + 1],
-                    )
-                v = late.tile([P, C], F32, tag="v", bufs=2)
-                for h in range(HALVES):
-                    nc.vector.scalar_tensor_tensor(
-                        out=v[:, half(h)], in0=ub[:, half(h)], scalar=neg_mean[:], in1=g_all[:, half(h)],
-                        op0=ALU.add, op1=ALU.mult,
-                    )
-                var_eps = late.tile([P, 1], F32, tag="var_eps_out", bufs=2)
-                nc.vector.tensor_scalar(
-                    out=var_eps[:], in0=var[:, 0:1], scalar1=var[:, 1:2], scalar2=EPS, op0=ALU.add, op1=ALU.add
+
+            def add_edge(a, h):
+                nc.vector.scalar_tensor_tensor(
+                    out=v[a][:, half(h)], in0=v[a][:, half(h)], scalar=rstd["out", a][:], in1=edge_b[:, a, half(h)],
+                    op0=ALU.mult, op1=ALU.add,
                 )
-                rstd = inverse_root(var_eps)
-                log = late.tile([P, C], F32, tag="log", bufs=2)
-                for h in range(HALVES):
-                    nc.vector.scalar_tensor_tensor(
-                        out=v[:, half(h)], in0=v[:, half(h)], scalar=rstd[:], in1=edge_b[:, a, half(h)],
-                        op0=ALU.mult, op1=ALU.add,
-                    )
-                    nc.scalar.activation(out=log[:, half(h)], in_=v[:, half(h)], func=ACT.Sigmoid, scale=-1.0)
-                vs.append(v)
-                logs.append(log)
+
+            sum_directions(0, 0)
+            sum_directions(1, 0)
+            sum_directions(0, 1)
+            quantise_gated(1, 1)
+            sum_directions(1, 1)
+            for h in range(HALVES):
+                add_bias(0, h)
+            out_stats(0)
+            add_bias(1, 0)
+            out_scale(0)
+            add_bias(1, 1)
+            out_stats(1)
+            centre_times_gain(0, 0)
+            out_scale(1)
+            centre_times_gain(0, 1)
+            for h in range(HALVES):
+                centre_times_gain(1, h)
             for a in range(A):
                 for h in range(HALVES):
-                    nc.scalar.activation(out=logs[a][:, half(h)], in_=logs[a][:, half(h)], func=ACT.Ln, bias=tiny[:])
+                    add_edge(a, h)
+                    nc.scalar.activation(out=log[a][:, half(h)], in_=v[a][:, half(h)], func=ACT.Sigmoid, scale=-1.0)
+            for a in range(A):
+                for h in range(HALVES):
+                    nc.scalar.activation(out=log[a][:, half(h)], in_=log[a][:, half(h)], func=ACT.Ln, bias=tiny[:])
                     nc.vector.scalar_tensor_tensor(
-                        out=logs[a][:, half(h)], in0=logs[a][:, half(h)], scalar=-1.0, in1=vs[a][:, half(h)],
+                        out=log[a][:, half(h)], in0=log[a][:, half(h)], scalar=-1.0, in1=v[a][:, half(h)],
                         op0=ALU.mult, op1=ALU.max,
                     )
-                    nc.sync.dma_start(out=out[a * P : (a + 1) * P, half(h)], in_=logs[a][:, half(h)])
+                    nc.sync.dma_start(out=out[a * P : (a + 1) * P, half(h)], in_=log[a][:, half(h)])

@@ -49,6 +49,8 @@ def tile_comformerconvedgelayer_pb_kernel(
         make_identity(nc, ident_f32[:])
         ident_bf = keep.tile([P, P], BF16)
         make_identity(nc, ident_bf[:])
+        b_row = keep.tile([P, C], BF16)
+        nc.gpsimd.memset(b_row[:], 0.0)
         neg_half = keep.tile([P, 1], F32)
         nc.vector.memset(neg_half[:], -0.5)
         tiny = keep.tile([P, 1], F32)
@@ -57,6 +59,7 @@ def tile_comformerconvedgelayer_pb_kernel(
         nc.vector.memset(vec_rows[:], 0.0)
         for i, vec in enumerate((bq, bk2, bm2, g_att, b_att)):
             nc.scalar.dma_start(out=vec_rows[i * J : (i + 1) * J, :], in_=vec.rearrange("(j p) -> j p", p=P))
+        nc.scalar.dma_start(out=b_row[0:1, :], in_=b_bn.rearrange("(o c) -> o c", o=1))
         chan = keep.tile([P, 5 * J], F32)
         warm = keep.tile([P, 1], F32)
         nc.scalar.activation(out=warm[:], in_=neg_half[:], func=ACT.Sigmoid)
@@ -74,13 +77,12 @@ def tile_comformerconvedgelayer_pb_kernel(
         g_scales = keep.tile([P, A, PASSES, T * P], U8, align_bytes=64)
         w_codes = {}
         w_scales = {}
-        qbT = keep.tile([P, J, E], F32, tag="qbT_then_edge_b")
+        qbT = keep.tile([P, J, E], F32)
         alphaT = [keep.tile([P, J, T, P], F32, name="alphaT%d" % a) for a in range(A)]
         sigT = [keep.tile([P, J, T * P], F32, name="sigT%d" % a) for a in range(A)]
         gated = [keep.tile([P, J, T, P], BF16, name="gated%d" % a) for a in range(A)]
         bc_all = keep.tile([P, C], BF16)
         g_all = keep.tile([P, C], BF16)
-        b_all = keep.tile([P, C], BF16)
         acc = {}
         grouped = {}
         stats = {}
@@ -247,7 +249,6 @@ def tile_comformerconvedgelayer_pb_kernel(
             load_rows("m", h_m, 1)
             load_weight("m", Wm2, True)
             load_weight("c", Wc, False)
-            nc.sync.dma_start(out=b_all[:], in_=b_bn.partition_broadcast(P))
             nc.sync.dma_start(out=bc_all[:], in_=bc.partition_broadcast(P))
             nc.sync.dma_start(out=g_all[:], in_=g_bn.partition_broadcast(P))
 
@@ -380,10 +381,6 @@ def tile_comformerconvedgelayer_pb_kernel(
                     normalise(1, t - 1)
             normalise(1, T - 1)
 
-            edge_b = keep.tile([P, A, C], F32, tag="qbT_then_edge_b")
-            for a in range(A):
-                nc.gpsimd.tensor_tensor(out=edge_b[:, a, :], in0=edge_raw[:, a, :], in1=b_all[:], op=ALU.add)
-
             regroup("c", 0, 1, True)
             quantise_piece("c", 0, 0)
             gate_edge_tile(0)
@@ -416,33 +413,69 @@ def tile_comformerconvedgelayer_pb_kernel(
                             stop=(g == PASSES - 1 and t == T - 1),
                         )
 
+            ub = [late.tile([P, C], F32, name="ub%d" % a) for a in range(A)]
             v = [late.tile([P, C], F32, name="v%d" % a) for a in range(A)]
             log = [late.tile([P, C], F32, name="log%d" % a) for a in range(A)]
+            squares = late.tile([P, A, C], F32)
+            sums = {}
+            neg_mean = {}
+            neg_mean_root = {}
+            var = {}
 
-            def add_bias(a, h):
-                nc.vector.scalar_tensor_tensor(
-                    out=v[a][:, half(h)], in0=bc_all[:, half(h)], scalar=float(T), in1=acc["u", a][h][:],
-                    op0=ALU.mult, op1=ALU.add,
-                )
-
-            def out_stats(a):
-                stats["out", a] = keep.tile([P, HALVES, 6], F32, tag="stats", bufs=4, name="stats")
+            def edge_plus_b(a):
+                acc["edge_b", a] = [bank("edge_b%d" % h) for h in range(HALVES)]
                 for h in range(HALVES):
-                    nc.vector.bn_stats(out=stats["out", a][:, h, :], in_=v[a][:, half(h)])
+                    nc.tensor.matmul(
+                        out=acc["edge_b", a][h][:], lhsT=ident_bf[:], rhs=edge_raw[:, a, half(h)], start=True, stop=False
+                    )
+                    nc.tensor.matmul(
+                        out=acc["edge_b", a][h][:], lhsT=ident_bf[:, 0:1].to_broadcast([P, P]), rhs=b_row[:, half(h)],
+                        start=False, stop=True,
+                    )
 
-            def out_scale(a):
-                aggregate(("out", a))
-                inverse_std(("out", a), EPS)
+            def add_bias(a):
+                sums[a] = late.tile([P, HALVES], F32, name="sums%d" % a)
+                for h in range(HALVES):
+                    nc.vector.scalar_tensor_tensor(
+                        out=ub[a][:, half(h)], in0=bc_all[:, half(h)], scalar=float(T), in1=acc["u", a][h][:],
+                        op0=ALU.mult, op1=ALU.add, accum_out=sums[a][:, h : h + 1],
+                    )
 
-            def centre_times_gain(a, h):
-                nc.vector.scalar_tensor_tensor(
-                    out=v[a][:, half(h)], in0=v[a][:, half(h)], scalar=mean_var["out", a][:, 0:1],
-                    in1=g_all[:, half(h)], op0=ALU.subtract, op1=ALU.mult,
+            def out_mean(a):
+                neg_mean[a] = late.tile([P, 1], F32, name="neg_mean%d" % a)
+                neg_mean_root[a] = late.tile([P, 1], F32, name="neg_mean_root%d" % a)
+                for dst, factor in ((neg_mean[a], -1.0 / C), (neg_mean_root[a], -1.0 / (C * C ** 0.5))):
+                    nc.gpsimd.tensor_scalar(
+                        out=dst[:], in0=sums[a][:, 0:1], scalar1=sums[a][:, 1:2], scalar2=factor,
+                        op0=ALU.add, op1=ALU.mult,
+                    )
+
+            def out_var(a):
+                var[a] = late.tile([P, HALVES], F32, name="var%d" % a)
+                for h in range(HALVES):
+                    nc.scalar.activation(
+                        out=squares[:, a, half(h)], in_=ub[a][:, half(h)], func=ACT.Square,
+                        scale=C ** -0.5, bias=neg_mean_root[a][:], accum_out=var[a][:, h : h + 1],
+                    )
+
+            def out_rstd(a):
+                var_eps = late.tile([P, 1], F32, name="var_eps%d" % a)
+                nc.gpsimd.tensor_scalar(
+                    out=var_eps[:], in0=var[a][:, 0:1], scalar1=var[a][:, 1:2], scalar2=EPS, op0=ALU.add, op1=ALU.add
                 )
+                rstd["out", a] = late.tile([P, 1], F32, name="rstd_out%d" % a)
+                nc.gpsimd.tensor_tensor(out=rstd["out", a][:], in0=var_eps[:], in1=neg_half[:], op=ALU.pow)
+
+            def centre_times_gain(a):
+                for h in range(HALVES):
+                    nc.vector.scalar_tensor_tensor(
+                        out=v[a][:, half(h)], in0=ub[a][:, half(h)], scalar=neg_mean[a][:], in1=g_all[:, half(h)],
+                        op0=ALU.add, op1=ALU.mult,
+                    )
 
             def add_edge(a, h):
                 nc.vector.scalar_tensor_tensor(
-                    out=v[a][:, half(h)], in0=v[a][:, half(h)], scalar=rstd["out", a][:], in1=edge_b[:, a, half(h)],
+                    out=v[a][:, half(h)], in0=v[a][:, half(h)], scalar=rstd["out", a][:], in1=acc["edge_b", a][h][:],
                     op0=ALU.mult, op1=ALU.add,
                 )
 
@@ -451,18 +484,17 @@ def tile_comformerconvedgelayer_pb_kernel(
             sum_directions(0, 1)
             quantise_gated(1, 1)
             sum_directions(1, 1)
-            for h in range(HALVES):
-                add_bias(0, h)
-            out_stats(0)
-            add_bias(1, 0)
-            out_scale(0)
-            add_bias(1, 1)
-            out_stats(1)
-            centre_times_gain(0, 0)
-            out_scale(1)
-            centre_times_gain(0, 1)
-            for h in range(HALVES):
-                centre_times_gain(1, h)
+            for a in range(A):
+                edge_plus_b(a)
+            for a in range(A):
+                add_bias(a)
+                out_mean(a)
+            out_var(0)
+            centre_times_gain(0)
+            out_var(1)
+            out_rstd(0)
+            centre_times_gain(1)
+            out_rstd(1)
             for a in range(A):
                 for h in range(HALVES):
                     add_edge(a, h)

@@ -49,8 +49,6 @@ def tile_comformerconvedgelayer_pb_kernel(
         make_identity(nc, ident_f32[:])
         ident_bf = keep.tile([P, P], BF16)
         make_identity(nc, ident_bf[:])
-        b_row = keep.tile([P, C], BF16)
-        nc.gpsimd.memset(b_row[:], 0.0)
         neg_half = keep.tile([P, 1], F32)
         nc.vector.memset(neg_half[:], -0.5)
         tiny = keep.tile([P, 1], F32)
@@ -59,8 +57,9 @@ def tile_comformerconvedgelayer_pb_kernel(
         nc.vector.memset(vec_rows[:], 0.0)
         for i, vec in enumerate((bq, bk2, bm2, g_att, b_att)):
             nc.scalar.dma_start(out=vec_rows[i * J : (i + 1) * J, :], in_=vec.rearrange("(j p) -> j p", p=P))
-        nc.scalar.dma_start(out=b_row[0:1, :], in_=b_bn.rearrange("(o c) -> o c", o=1))
         chan = keep.tile([P, 5 * J], F32)
+        b_row = keep.tile([P, C], BF16)
+        nc.vector.memset(b_row[:], 0.0)
         warm = keep.tile([P, 1], F32)
         nc.scalar.activation(out=warm[:], in_=neg_half[:], func=ACT.Sigmoid)
 
@@ -249,6 +248,7 @@ def tile_comformerconvedgelayer_pb_kernel(
             load_rows("m", h_m, 1)
             load_weight("m", Wm2, True)
             load_weight("c", Wc, False)
+            nc.sync.dma_start(out=b_row[0:1, :], in_=b_bn.rearrange("(o c) -> o c", o=1))
             nc.sync.dma_start(out=bc_all[:], in_=bc.partition_broadcast(P))
             nc.sync.dma_start(out=g_all[:], in_=g_bn.partition_broadcast(P))
 
@@ -361,8 +361,8 @@ def tile_comformerconvedgelayer_pb_kernel(
             for j in (J - 2, J - 1):
                 times_query(1, j)
 
-            transpose_alpha(1, 0)
-            transpose_alpha(1, 1)
+            for t in range(T):
+                transpose_alpha(1, t)
             quantise_directions("m", 1)
             regroup("m", 1, 0, False)
             new_weight("c")
@@ -376,7 +376,6 @@ def tile_comformerconvedgelayer_pb_kernel(
                 if t == 0:
                     for j in range(J):
                         gate_weights(0, j)
-                    transpose_alpha(1, 2)
                 else:
                     normalise(1, t - 1)
             normalise(1, T - 1)

@@ -336,6 +336,7 @@ def tile_comformerconvedgelayer_pb_kernel(
 
             new_weight("m")
             regroup("m", 0, 0, True)
+            regroup("m", 1, 0, True)
             for j in range(J):
                 times_query(0, j)
             for j in range(2):
@@ -351,7 +352,7 @@ def tile_comformerconvedgelayer_pb_kernel(
                 if t == 0:
                     quantise_directions("m", 0)
                 else:
-                    quantise_piece("m", 0, t - 1)
+                    quantise_piece("m", t - 1, 0)
                 row_scale(0, t)
                 if t == 0:
                     directions_to_words("m", 1)
@@ -364,12 +365,11 @@ def tile_comformerconvedgelayer_pb_kernel(
             for t in range(T):
                 transpose_alpha(1, t)
             quantise_directions("m", 1)
-            regroup("m", 1, 0, False)
             new_weight("c")
             for t in range(T):
                 row_stats(1, t)
                 if t < 2:
-                    quantise_piece("m", 1, t)
+                    quantise_piece("m", t, 1)
                 else:
                     regroup("c", 0, 0, False)
                 row_scale(1, t)

@@ -55,13 +55,14 @@ def tile_comformerconvedgelayer_pb_kernel(
         nc.vector.memset(tiny[:], TINY)
         vec_rows = keep.tile([P, P], BF16)
         nc.vector.memset(vec_rows[:], 0.0)
-        for i, vec in enumerate((bq, bk2, bm2, g_att, b_att)):
-            nc.scalar.dma_start(out=vec_rows[i * J : (i + 1) * J, :], in_=vec.rearrange("(j p) -> j p", p=P))
         chan = keep.tile([P, 5 * J], F32)
         b_row = keep.tile([P, C], BF16)
         nc.vector.memset(b_row[:], 0.0)
         warm = keep.tile([P, 1], F32)
-        nc.scalar.activation(out=warm[:], in_=neg_half[:], func=ACT.Sigmoid)
+
+        def warm_up():
+            nc.scalar.activation(out=warm[:], in_=neg_half[:], func=ACT.Sigmoid)
+
 
         def chan_col(base, j):
             return chan[:, base + j : base + j + 1]
@@ -77,12 +78,13 @@ def tile_comformerconvedgelayer_pb_kernel(
         w_codes = {}
         w_scales = {}
         qbT = keep.tile([P, J, E], F32)
-        alphaT = [keep.tile([P, J, T, P], F32, name="alphaT%d" % a) for a in range(A)]
+        alphaT = [keep.tile([P, J, T, P], F32, tag="alphaT", bufs=2, name="alphaT") for a in range(A)]
         sigT = [keep.tile([P, J, T * P], F32, name="sigT%d" % a) for a in range(A)]
         gated = [keep.tile([P, J, T, P], BF16, name="gated%d" % a) for a in range(A)]
         bc_all = keep.tile([P, C], BF16)
         g_all = keep.tile([P, C], BF16)
         acc = {}
+        raw = {}
         grouped = {}
         stats = {}
         rstd = {}
@@ -90,9 +92,128 @@ def tile_comformerconvedgelayer_pb_kernel(
         mean_var = {}
         ys = {}
 
+        def load_rows(name, x, a):
+            raw[name, a] = keep.tile([P, T, C], BF16, tag="rows_raw", bufs=3, name="rows_raw")
+            nc.sync.dma_start(out=raw[name, a][:], in_=x[a * P : (a + 1) * P, :, :])
+
+        def new_raw(name, g):
+            raw[name, g] = keep.tile([P, PACK, C], BF16, tag="w_raw", bufs=4, name="w_raw")
+
+        def load_pairs(name, w, g):
+            new_raw(name, g)
+            nc.sync.dma_start(
+                out=raw[name, g][:].rearrange("p (u e) w -> p u (e w)", u=2),
+                in_=w[g * K_PASS : (g + 1) * K_PASS, :].rearrange("(u p e) w -> p u (e w)", u=2, p=P),
+            )
+
+        def load_rows_of_128(name, w, g):
+            new_raw(name, g)
+            nc.sync.dma_start(
+                out=raw[name, g][:], in_=w[g * K_PASS : (g + 1) * K_PASS, :].rearrange("(f p) w -> p f w", p=P)
+            )
+
+        def raw_columns(name, g, lo, hi):
+            return raw[name, g][:, :, lo:hi]
+
+        def load_edge():
+            nc.sync.dma_start(out=edge_raw[:], in_=edge.rearrange("(a p) c -> p a c", p=P))
+
+        def load_x(name, a):
+            load_rows(name + "x", h_k if name == "k" else h_m, a)
+
+        def load_w(name, g):
+            if name == "c":
+                load_rows_of_128(name, Wc, g)
+            else:
+                load_pairs(name, {"q": Wq, "k": Wk2, "m": Wm2}[name], g)
+
+        def load_columns():
+            for i, vec in enumerate((bq, bk2, bm2, g_att, b_att)):
+                nc.scalar.dma_start(out=vec_rows[i * J : (i + 1) * J, :], in_=vec.rearrange("(j p) -> j p", p=P))
+
+        def load_vectors():
+            nc.sync.dma_start(out=b_row[0:1, :], in_=b_bn.rearrange("(o c) -> o c", o=1))
+            nc.sync.dma_start(out=bc_all[:], in_=bc.partition_broadcast(P))
+            nc.sync.dma_start(out=g_all[:], in_=g_bn.partition_broadcast(P))
+
+        def rows_to_words(name, rt, words):
+            wordsT = psum.tile([P, PASSES * 2, P], F32, tag="bank", name="wordsT")
+            for s in range(PASSES * 2):
+                nc.tensor.transpose(wordsT[:, s, :], words[:, block(s)], ident_f32[:])
+            grouped[name, rt] = keep.tile(
+                [P, PASSES, P, PACK], BF16, tag="x_grouped", bufs=4, name="x_grouped", align_bytes=64
+            )
+            nc.scalar.copy(
+                out=grouped[name, rt][:].bitcast(F32), in_=wordsT[:].rearrange("p (g u) r -> p g r u", u=2)
+            )
+
+        def quantise_rows(name, rt):
+            nc.vector.quantize_mx(
+                out=x_codes[name][:, rt, :].bitcast(FP8X4),
+                scales=x_scales[name][:, rt, :],
+                in_=grouped[name, rt][:].rearrange("p g r f -> p (g r f)"),
+            )
+
+        def direction_to_words(name, a, t):
+            rows_to_words(name, a * T + t, raw[name + "x", a][:, t, :].bitcast(F32))
+
         def new_weight(name):
-            w_codes[name] = keep.tile([P, PASSES, C], U32, tag="w_codes", bufs=3, name="codes_" + name, align_bytes=64)
-            w_scales[name] = keep.tile([P, PASSES, C], U8, tag="w_scales", bufs=3, name="scales_" + name, align_bytes=64)
+            w_codes[name] = keep.tile([P, PASSES, C], U32, tag="w_codes", bufs=3, name="w_codes", align_bytes=64)
+            w_scales[name] = keep.tile([P, PASSES, C], U8, tag="w_scales", bufs=3, name="w_scales", align_bytes=64)
+
+        def new_grouped(name, g, h):
+            grouped[name, g, h] = keep.tile(
+                [P, BANK, PACK], BF16, tag="w_grouped", bufs=5, name="w_grouped", align_bytes=64
+            )
+
+        def four_columns(name, g, h, lo, hi):
+            dst = grouped[name, g, h][:, lo:hi, :].rearrange("p (c i) f -> p c f i", i=4)
+            src = raw_columns(name, g, h * BANK + lo, h * BANK + hi).rearrange("p f (c i) -> p c f i", i=4)
+            return dst, src
+
+        def on_vector(name, g, h):
+            new_grouped(name, g, h)
+            dst, src = four_columns(name, g, h, 0, BANK)
+            nc.vector.tensor_copy(out=dst, in_=src)
+
+        def on_scalar(name, g, h):
+            new_grouped(name, g, h)
+            dst, src = four_columns(name, g, h, 0, BANK)
+            nc.scalar.copy(out=dst, in_=src)
+
+        def go():
+            token = keep.tile([P, 1], F32, tag="token", bufs=4, name="token")
+            nc.vector.memset(token[:], 1.0)
+            return token
+
+        def half_on_gpsimd(name, g, h, part, wait):
+            if part == 0:
+                new_grouped(name, g, h)
+            lo = part * BANK // 2
+            nc.gpsimd.tensor_scalar(
+                out=grouped[name, g, h][:, lo : lo + BANK // 2, :],
+                in0=raw_columns(name, g, h * BANK + lo, h * BANK + lo + BANK // 2).rearrange("p f w -> p w f"),
+                scalar1=go()[:] if wait else 1.0, scalar2=0.0, op0=ALU.mult, op1=ALU.add,
+            )
+
+        def on_tensor(name, g, h):
+            new_grouped(name, g, h)
+            for lo in (0, BANK // 2):
+                words = psum.tile([P, BANK // 2, PACK], BF16, tag="bank", name="words")
+                for c in range(2):
+                    first = h * BANK + lo + c * P
+                    nc.tensor.matmul(
+                        out=words[:, block(c), :], lhsT=ident_bf[:],
+                        rhs=raw_columns(name, g, first, first + P).rearrange("p f n -> p n f"), start=True, stop=True,
+                    )
+                nc.scalar.copy(out=grouped[name, g, h][:, lo : lo + BANK // 2, :], in_=words[:])
+
+        def quantise_piece(name, g, h):
+            nc.vector.quantize_mx(
+                out=w_codes[name][:, g, half(h)].bitcast(FP8X4),
+                scales=w_scales[name][:, g, half(h)],
+                in_=grouped[name, g, h][:].rearrange("p w f -> p (w f)"),
+            )
 
         def mx_group(out_cols, w, j, x, rt):
             for g in range(PASSES):
@@ -107,16 +228,12 @@ def tile_comformerconvedgelayer_pb_kernel(
                 )
 
         def inverse_std(key, eps):
-            var_eps = keep.tile([P, 1], F32, tag="var_eps", bufs=4)
+            var_eps = keep.tile([P, 1], F32, tag="var_eps", bufs=4, name="var_eps")
             nc.gpsimd.tensor_scalar(
                 out=var_eps[:], in0=mean_var[key][:, 1:2], scalar1=eps, scalar2=1.0, op0=ALU.add, op1=ALU.mult
             )
             rstd[key] = keep.tile([P, 1], F32, tag="rstd", bufs=4, name="rstd")
             nc.gpsimd.tensor_tensor(out=rstd[key][:], in0=var_eps[:], in1=neg_half[:], op=ALU.pow)
-
-        def aggregate(key):
-            mean_var[key] = keep.tile([P, 2], F32, tag="mean_var", bufs=4, name="mean_var")
-            nc.vector.bn_aggr(out=mean_var[key][:], in_=stats[key][:].rearrange("p h s -> p (h s)"))
 
         def query_products(j):
             acc["q", j] = bank("qT")
@@ -156,7 +273,8 @@ def tile_comformerconvedgelayer_pb_kernel(
                 nc.vector.bn_stats(out=stats[a, t][:, h, :], in_=acc["alpha", a, t][h][:])
 
         def row_scale(a, t):
-            aggregate((a, t))
+            mean_var[a, t] = keep.tile([P, 2], F32, tag="mean_var", bufs=4, name="mean_var")
+            nc.vector.bn_aggr(out=mean_var[a, t][:], in_=stats[a, t][:].rearrange("p h s -> p (h s)"))
             inverse_std((a, t), C * EPS)
             shift[a, t] = keep.tile([P, 1], F32, tag="shift", bufs=4, name="shift")
             nc.gpsimd.tensor_scalar(
@@ -194,14 +312,16 @@ def tile_comformerconvedgelayer_pb_kernel(
                 op1=ALU.mult,
             )
 
-        def regroup_gated(a, g):
+        def regroup_gated(a, g, gpsimd):
             grouped["g", a, g] = keep.tile(
                 [P, T * P, PACK], BF16, tag="gated_grouped", bufs=2, name="gated_grouped", align_bytes=64
             )
-            nc.vector.tensor_copy(
-                out=grouped["g", a, g][:],
-                in_=gated[a][:, g * PACK : (g + 1) * PACK, :, :].rearrange("p f t e -> p (t e) f"),
-            )
+            dst = grouped["g", a, g][:]
+            src = gated[a][:, g * PACK : (g + 1) * PACK, :, :].rearrange("p f t e -> p (t e) f")
+            if gpsimd:
+                nc.gpsimd.tensor_scalar(out=dst, in0=src, scalar1=1.0, scalar2=0.0, op0=ALU.mult, op1=ALU.add)
+            else:
+                nc.vector.tensor_copy(out=dst, in_=src)
 
         def quantise_gated(a, g):
             for lo, hi in ((0, 2 * P), (2 * P, 3 * P)):
@@ -211,298 +331,257 @@ def tile_comformerconvedgelayer_pb_kernel(
                     in_=grouped["g", a, g][:, lo:hi, :].rearrange("p r f -> p (r f)"),
                 )
 
-        def gate_edge_tile(a):
-            for j in range(J):
-                gate_messages(a, j)
-                if j == PACK:
-                    regroup_gated(a, 0)
-                if j == PACK + 2:
-                    quantise_gated(a, 0)
+        ub = {}
+        v = {}
+        log = {}
+        squares = keep.tile([P, BANK], F32)
+        sums = {}
+        neg_mean = {}
+        neg_mean_root = {}
+        var = {}
 
-        with tc.tile_pool(name="stage", bufs=1) as stage:
-            rows_raw = {}
-            w_raw = {}
-
-            def load_rows(name, x, a):
-                rows_raw[name, a] = stage.tile([P, T, C], BF16, tag="rows_raw", bufs=3, name="rows_raw")
-                nc.sync.dma_start(out=rows_raw[name, a][:], in_=x[a * P : (a + 1) * P, :, :])
-
-            def load_weight(name, w, pairs):
-                for g in range(PASSES):
-                    w_raw[name, g] = stage.tile([P, PACK, C], BF16, tag="w_raw", bufs=4, name="w_raw")
-                    rows = w[g * K_PASS : (g + 1) * K_PASS, :]
-                    if pairs:
-                        nc.sync.dma_start(
-                            out=w_raw[name, g][:].rearrange("p (u e) w -> p u (e w)", u=2),
-                            in_=rows.rearrange("(u p e) w -> p u (e w)", u=2, p=P),
-                        )
-                    else:
-                        nc.sync.dma_start(out=w_raw[name, g][:], in_=rows.rearrange("(f p) w -> p f w", p=P))
-
-            nc.sync.dma_start(out=edge_raw[:], in_=edge.rearrange("(a p) c -> p a c", p=P))
-            load_weight("q", Wq, True)
-            load_rows("k", h_k, 0)
-            load_weight("k", Wk2, True)
-            load_rows("k", h_k, 1)
-            load_rows("m", h_m, 0)
-            load_rows("m", h_m, 1)
-            load_weight("m", Wm2, True)
-            load_weight("c", Wc, False)
-            nc.sync.dma_start(out=b_row[0:1, :], in_=b_bn.rearrange("(o c) -> o c", o=1))
-            nc.sync.dma_start(out=bc_all[:], in_=bc.partition_broadcast(P))
-            nc.sync.dma_start(out=g_all[:], in_=g_bn.partition_broadcast(P))
-
-            def rows_to_words(name, rt, words):
-                wordsT = psum.tile([P, PASSES * 2, P], F32, tag="bank")
-                for s in range(PASSES * 2):
-                    nc.tensor.transpose(wordsT[:, s, :], words[:, block(s)], ident_f32[:])
-                grouped[name, rt] = stage.tile(
-                    [P, PASSES, P, PACK], BF16, tag="x_grouped", bufs=3, name="x_grouped", align_bytes=64
-                )
-                nc.scalar.copy(
-                    out=grouped[name, rt][:].bitcast(F32), in_=wordsT[:].rearrange("p (g u) r -> p g r u", u=2)
-                )
-
-            def quantise_rows(name, rt):
-                nc.vector.quantize_mx(
-                    out=x_codes[name][:, rt, :].bitcast(FP8X4),
-                    scales=x_scales[name][:, rt, :],
-                    in_=grouped[name, rt][:].rearrange("p g r f -> p (g r f)"),
-                )
-
-            def directions_to_words(name, a):
+        def sum_directions(a, g):
+            if g == 0:
+                acc["u", a] = [bank("u%d" % h) for h in range(HALVES)]
+            for h in range(HALVES):
                 for t in range(T):
-                    rows_to_words(name, a * T + t, rows_raw[name, a][:, t, :].bitcast(F32))
+                    nc.tensor.matmul_mx(
+                        out=acc["u", a][h][:],
+                        lhsT=g_codes[:, a, g, block(t)].bitcast(FP8X4),
+                        lhsT_scale=g_scales[:, a, g, block(t)],
+                        rhs=w_codes["c"][:, g, half(h)].bitcast(FP8X4),
+                        rhs_scale=w_scales["c"][:, g, half(h)],
+                        start=(g == 0 and t == 0),
+                        stop=(g == PASSES - 1 and t == T - 1),
+                    )
 
-            def quantise_directions(name, a):
-                for t in range(T):
-                    quantise_rows(name, a * T + t)
-
-            def regroup(name, g, h, on_scalar):
-                grouped[name, g, h] = stage.tile(
-                    [P, BANK, PACK], BF16, tag="w_grouped", bufs=4, name="w_grouped", align_bytes=64
+        def edge_plus_b(a):
+            acc["edge_b", a] = [bank("edge_b%d" % h) for h in range(HALVES)]
+            for h in range(HALVES):
+                nc.tensor.matmul(
+                    out=acc["edge_b", a][h][:], lhsT=ident_bf[:], rhs=edge_raw[:, a, half(h)], start=True, stop=False
                 )
-                dst = grouped[name, g, h][:].rearrange("p (c i) f -> p c f i", i=4)
-                src = w_raw[name, g][:, :, half(h)].rearrange("p f (c i) -> p c f i", i=4)
-                if on_scalar:
-                    nc.scalar.copy(out=dst, in_=src)
-                else:
-                    nc.vector.tensor_copy(out=dst, in_=src)
-
-            def quantise_piece(name, g, h):
-                nc.vector.quantize_mx(
-                    out=w_codes[name][:, g, half(h)].bitcast(FP8X4),
-                    scales=w_scales[name][:, g, half(h)],
-                    in_=grouped[name, g, h][:].rearrange("p w f -> p (w f)"),
+                nc.tensor.matmul(
+                    out=acc["edge_b", a][h][:], lhsT=ident_bf[:, 0:1].to_broadcast([P, P]), rhs=b_row[:, half(h)],
+                    start=False, stop=True,
                 )
 
-            for a in range(A):
-                rows_to_words("e", a, edge_raw[:, a, :].bitcast(F32))
-            vec_cols = psum.tile([P, P], BF16, tag="bank")
-            nc.tensor.transpose(vec_cols[:], vec_rows[:], ident_bf[:])
-            for a in range(A):
-                quantise_rows("e", a)
-            nc.vector.tensor_copy(out=chan[:], in_=vec_cols[:, 0 : 5 * J])
-            new_weight("q")
-            for g in range(PASSES):
-                regroup("q", g, 0, False)
-                regroup("q", g, 1, True)
-            for g in range(PASSES):
-                for h in range(HALVES):
-                    quantise_piece("q", g, h)
-            directions_to_words("k", 0)
-            for j in range(J):
-                query_products(j)
-
-            new_weight("k")
-            regroup("k", 0, 0, False)
-            regroup("k", 0, 1, True)
-            quantise_directions("k", 0)
-            for j in range(J):
-                add_query_bias(j)
-            regroup("k", 1, 0, False)
-            quantise_piece("k", 0, 0)
-            regroup("k", 1, 1, False)
-            quantise_piece("k", 0, 1)
-            quantise_piece("k", 1, 0)
-            directions_to_words("k", 1)
-            directions_to_words("m", 0)
-            for j in range(J // 2):
-                key_products(0, j)
-            quantise_piece("k", 1, 1)
-            quantise_directions("k", 1)
-            for j in range(J // 2, J):
-                key_products(0, j)
-
-            new_weight("m")
-            regroup("m", 0, 0, True)
-            regroup("m", 1, 0, True)
-            for j in range(J):
-                times_query(0, j)
-            for j in range(2):
-                key_products(1, j)
-
-            for t in range(T):
-                transpose_alpha(0, t)
-                for j in (2 * t + 2, 2 * t + 3):
-                    key_products(1, j)
-                for j in (2 * t, 2 * t + 1):
-                    times_query(1, j)
-                row_stats(0, t)
-                if t == 0:
-                    quantise_directions("m", 0)
-                else:
-                    quantise_piece("m", t - 1, 0)
-                row_scale(0, t)
-                if t == 0:
-                    directions_to_words("m", 1)
-                else:
-                    regroup("m", t - 1, 1, True)
-                normalise(0, t)
-            for j in (J - 2, J - 1):
-                times_query(1, j)
-
-            for t in range(T):
-                transpose_alpha(1, t)
-            quantise_directions("m", 1)
-            new_weight("c")
-            for t in range(T):
-                row_stats(1, t)
-                if t < 2:
-                    quantise_piece("m", t, 1)
-                else:
-                    regroup("c", 0, 0, False)
-                row_scale(1, t)
-                if t == 0:
-                    for j in range(J):
-                        gate_weights(0, j)
-                else:
-                    normalise(1, t - 1)
-            normalise(1, T - 1)
-
-            regroup("c", 0, 1, True)
-            quantise_piece("c", 0, 0)
-            gate_edge_tile(0)
-            regroup_gated(0, 1)
-            for j in range(J):
-                gate_weights(1, j)
-            regroup("c", 1, 0, True)
-            regroup("c", 1, 1, True)
-            quantise_piece("c", 0, 1)
-            quantise_gated(0, 1)
-            gate_edge_tile(1)
-            quantise_piece("c", 1, 0)
-            regroup_gated(1, 1)
-            quantise_piece("c", 1, 1)
-
-        with tc.tile_pool(name="late", bufs=1, reuse_waits="tile") as late:
-
-            def sum_directions(a, g):
-                if g == 0:
-                    acc["u", a] = [bank("u%d" % h) for h in range(HALVES)]
-                for t in range(T):
-                    for h in range(HALVES):
-                        nc.tensor.matmul_mx(
-                            out=acc["u", a][h][:],
-                            lhsT=g_codes[:, a, g, block(t)].bitcast(FP8X4),
-                            lhsT_scale=g_scales[:, a, g, block(t)],
-                            rhs=w_codes["c"][:, g, half(h)].bitcast(FP8X4),
-                            rhs_scale=w_scales["c"][:, g, half(h)],
-                            start=(g == 0 and t == 0),
-                            stop=(g == PASSES - 1 and t == T - 1),
-                        )
-
-            ub = [late.tile([P, C], F32, name="ub%d" % a) for a in range(A)]
-            v = [late.tile([P, C], F32, name="v%d" % a) for a in range(A)]
-            log = [late.tile([P, C], F32, name="log%d" % a) for a in range(A)]
-            squares = late.tile([P, A, C], F32)
-            sums = {}
-            neg_mean = {}
-            neg_mean_root = {}
-            var = {}
-
-            def edge_plus_b(a):
-                acc["edge_b", a] = [bank("edge_b%d" % h) for h in range(HALVES)]
-                for h in range(HALVES):
-                    nc.tensor.matmul(
-                        out=acc["edge_b", a][h][:], lhsT=ident_bf[:], rhs=edge_raw[:, a, half(h)], start=True, stop=False
-                    )
-                    nc.tensor.matmul(
-                        out=acc["edge_b", a][h][:], lhsT=ident_bf[:, 0:1].to_broadcast([P, P]), rhs=b_row[:, half(h)],
-                        start=False, stop=True,
-                    )
-
-            def add_bias(a):
-                sums[a] = late.tile([P, HALVES], F32, name="sums%d" % a)
-                for h in range(HALVES):
-                    nc.vector.scalar_tensor_tensor(
-                        out=ub[a][:, half(h)], in0=bc_all[:, half(h)], scalar=float(T), in1=acc["u", a][h][:],
-                        op0=ALU.mult, op1=ALU.add, accum_out=sums[a][:, h : h + 1],
-                    )
-
-            def out_mean(a):
-                neg_mean[a] = late.tile([P, 1], F32, name="neg_mean%d" % a)
-                neg_mean_root[a] = late.tile([P, 1], F32, name="neg_mean_root%d" % a)
-                for dst, factor in ((neg_mean[a], -1.0 / C), (neg_mean_root[a], -1.0 / (C * C ** 0.5))):
-                    nc.gpsimd.tensor_scalar(
-                        out=dst[:], in0=sums[a][:, 0:1], scalar1=sums[a][:, 1:2], scalar2=factor,
-                        op0=ALU.add, op1=ALU.mult,
-                    )
-
-            def out_var(a):
-                var[a] = late.tile([P, HALVES], F32, name="var%d" % a)
-                for h in range(HALVES):
-                    nc.scalar.activation(
-                        out=squares[:, a, half(h)], in_=ub[a][:, half(h)], func=ACT.Square,
-                        scale=C ** -0.5, bias=neg_mean_root[a][:], accum_out=var[a][:, h : h + 1],
-                    )
-
-            def out_rstd(a):
-                var_eps = late.tile([P, 1], F32, name="var_eps%d" % a)
-                nc.gpsimd.tensor_scalar(
-                    out=var_eps[:], in0=var[a][:, 0:1], scalar1=var[a][:, 1:2], scalar2=EPS, op0=ALU.add, op1=ALU.add
-                )
-                rstd["out", a] = late.tile([P, 1], F32, name="rstd_out%d" % a)
-                nc.gpsimd.tensor_tensor(out=rstd["out", a][:], in0=var_eps[:], in1=neg_half[:], op=ALU.pow)
-
-            def centre_times_gain(a):
-                for h in range(HALVES):
-                    nc.vector.scalar_tensor_tensor(
-                        out=v[a][:, half(h)], in0=ub[a][:, half(h)], scalar=neg_mean[a][:], in1=g_all[:, half(h)],
-                        op0=ALU.add, op1=ALU.mult,
-                    )
-
-            def add_edge(a, h):
+        def add_bias(a):
+            late = keep.tile([P, 3, C], F32, tag="alphaT", bufs=2, name="late")
+            ub[a], v[a], log[a] = [late[:, i, :] for i in range(3)]
+            sums[a] = keep.tile([P, HALVES], F32, name="sums%d" % a)
+            for h in range(HALVES):
                 nc.vector.scalar_tensor_tensor(
-                    out=v[a][:, half(h)], in0=v[a][:, half(h)], scalar=rstd["out", a][:], in1=acc["edge_b", a][h][:],
-                    op0=ALU.mult, op1=ALU.add,
+                    out=ub[a][:, half(h)], in0=bc_all[:, half(h)], scalar=float(T), in1=acc["u", a][h][:],
+                    op0=ALU.mult, op1=ALU.add, accum_out=sums[a][:, h : h + 1],
                 )
 
-            sum_directions(0, 0)
-            sum_directions(1, 0)
-            sum_directions(0, 1)
-            quantise_gated(1, 1)
-            sum_directions(1, 1)
-            for a in range(A):
-                edge_plus_b(a)
-            for a in range(A):
-                add_bias(a)
-                out_mean(a)
-            out_var(0)
-            centre_times_gain(0)
-            out_var(1)
-            out_rstd(0)
-            centre_times_gain(1)
-            out_rstd(1)
-            for a in range(A):
-                for h in range(HALVES):
-                    add_edge(a, h)
-                    nc.scalar.activation(out=log[a][:, half(h)], in_=v[a][:, half(h)], func=ACT.Sigmoid, scale=-1.0)
-            for a in range(A):
-                for h in range(HALVES):
-                    nc.scalar.activation(out=log[a][:, half(h)], in_=log[a][:, half(h)], func=ACT.Ln, bias=tiny[:])
-                    nc.vector.scalar_tensor_tensor(
-                        out=log[a][:, half(h)], in0=log[a][:, half(h)], scalar=-1.0, in1=v[a][:, half(h)],
-                        op0=ALU.mult, op1=ALU.max,
-                    )
-                    nc.sync.dma_start(out=out[a * P : (a + 1) * P, half(h)], in_=log[a][:, half(h)])
+        def out_mean(a):
+            neg_mean[a] = keep.tile([P, 1], F32, name="neg_mean%d" % a)
+            neg_mean_root[a] = keep.tile([P, 1], F32, name="neg_mean_root%d" % a)
+            for dst, factor in ((neg_mean_root[a], -1.0 / (C * C ** 0.5)), (neg_mean[a], -1.0 / C)):
+                nc.gpsimd.tensor_scalar(
+                    out=dst[:], in0=sums[a][:, 0:1], scalar1=sums[a][:, 1:2], scalar2=factor,
+                    op0=ALU.add, op1=ALU.mult,
+                )
+
+        def out_var(a):
+            var[a] = keep.tile([P, HALVES], F32, name="var%d" % a)
+            for h in range(HALVES):
+                nc.scalar.activation(
+                    out=squares[:], in_=ub[a][:, half(h)], func=ACT.Square,
+                    scale=C ** -0.5, bias=neg_mean_root[a][:], accum_out=var[a][:, h : h + 1],
+                )
+
+        def out_rstd(a):
+            var_eps = keep.tile([P, 1], F32, name="out_var_eps%d" % a)
+            nc.gpsimd.tensor_scalar(
+                out=var_eps[:], in0=var[a][:, 0:1], scalar1=var[a][:, 1:2], scalar2=EPS, op0=ALU.add, op1=ALU.add
+            )
+            rstd["out", a] = keep.tile([P, 1], F32, name="rstd_out%d" % a)
+            nc.gpsimd.tensor_tensor(out=rstd["out", a][:], in0=var_eps[:], in1=neg_half[:], op=ALU.pow)
+
+        def centre_times_gain(a):
+            for h in range(HALVES):
+                nc.vector.scalar_tensor_tensor(
+                    out=v[a][:, half(h)], in0=ub[a][:, half(h)], scalar=neg_mean[a][:], in1=g_all[:, half(h)],
+                    op0=ALU.add, op1=ALU.mult,
+                )
+
+        def add_edge(a, h):
+            nc.vector.scalar_tensor_tensor(
+                out=v[a][:, half(h)], in0=v[a][:, half(h)], scalar=rstd["out", a][:], in1=acc["edge_b", a][h][:],
+                op0=ALU.mult, op1=ALU.add,
+            )
+
+        def sigmoid(a, h):
+            nc.scalar.activation(out=log[a][:, half(h)], in_=v[a][:, half(h)], func=ACT.Sigmoid, scale=-1.0)
+
+        def finish(a, h):
+            nc.scalar.activation(out=log[a][:, half(h)], in_=log[a][:, half(h)], func=ACT.Ln, bias=tiny[:])
+            nc.vector.scalar_tensor_tensor(
+                out=log[a][:, half(h)], in0=log[a][:, half(h)], scalar=-1.0, in1=v[a][:, half(h)],
+                op0=ALU.mult, op1=ALU.max,
+            )
+            nc.sync.dma_start(out=out[a * P : (a + 1) * P, half(h)], in_=log[a][:, half(h)])
+
+
+        load_columns()
+        warm_up()
+        load_edge()
+        load_w("q", 0)
+        load_w("q", 1)
+        load_x("k", 0)
+        load_w("k", 0)
+        load_w("k", 1)
+        load_x("k", 1)
+        load_x("m", 0)
+        load_x("m", 1)
+        load_w("m", 0)
+        load_w("m", 1)
+        load_w("c", 0)
+        load_w("c", 1)
+        load_vectors()
+
+        for a in range(A):
+            rows_to_words("e", a, edge_raw[:, a, :].bitcast(F32))
+        vec_cols = psum.tile([P, P], BF16, tag="bank", name="vec_cols")
+        nc.tensor.transpose(vec_cols[:], vec_rows[:], ident_bf[:])
+        nc.vector.tensor_copy(out=chan[:], in_=vec_cols[:, 0 : 5 * J])
+        for a in range(A):
+            quantise_rows("e", a)
+        new_weight("q")
+        on_vector("q", 0, 0)
+        on_scalar("q", 0, 1)
+        on_vector("q", 1, 0)
+        on_scalar("q", 1, 1)
+        quantise_piece("q", 0, 0)
+        quantise_piece("q", 0, 1)
+        quantise_piece("q", 1, 0)
+        quantise_piece("q", 1, 1)
+        for t in range(T):
+            direction_to_words("k", 0, t)
+        for j in range(J):
+            query_products(j)
+        new_weight("k")
+        on_vector("k", 0, 0)
+        on_scalar("k", 0, 1)
+        for t in range(T):
+            quantise_rows("k", t)
+        for j in range(J):
+            add_query_bias(j)
+        on_vector("k", 1, 0)
+        quantise_piece("k", 0, 0)
+        on_vector("k", 1, 1)
+        quantise_piece("k", 0, 1)
+        quantise_piece("k", 1, 0)
+        for t in range(T):
+            direction_to_words("k", 1, t)
+        for t in range(T):
+            direction_to_words("m", 0, t)
+        for j in range(J // 2):
+            key_products(0, j)
+        quantise_piece("k", 1, 1)
+        for t in range(T):
+            quantise_rows("k", T + t)
+        for j in range(J // 2, J):
+            key_products(0, j)
+        new_weight("m")
+        on_scalar("m", 0, 0)
+        on_scalar("m", 1, 0)
+        for j in range(J):
+            times_query(0, j)
+        for j in range(2):
+            key_products(1, j)
+        for t in range(T):
+            transpose_alpha(0, t)
+            for j in (2 * t + 2, 2 * t + 3):
+                key_products(1, j)
+            for j in (2 * t, 2 * t + 1):
+                times_query(1, j)
+            row_stats(0, t)
+            if t == 0:
+                for tt in range(T):
+                    quantise_rows("m", tt)
+            else:
+                quantise_piece("m", t - 1, 0)
+            row_scale(0, t)
+            if t < 2:
+                half_on_gpsimd("m", 1, 1, t, False)
+            if t == 0:
+                for tt in range(T):
+                    direction_to_words("m", 1, tt)
+            if t == 1:
+                on_scalar("m", 0, 1)
+            normalise(0, t)
+        for j in (J - 2, J - 1):
+            times_query(1, j)
+        for t in range(2):
+            transpose_alpha(1, t)
+        for t in range(T):
+            quantise_rows("m", T + t)
+        new_weight("c")
+        for t in range(T):
+            row_stats(1, t)
+            if t < 2:
+                quantise_piece("m", t, 1)
+            else:
+                on_vector("c", 0, 0)
+            row_scale(1, t)
+            if t == 0:
+                for j in range(4):
+                    gate_weights(0, j)
+                transpose_alpha(1, 2)
+            if t == 1:
+                normalise(1, 0)
+                for j in range(4, J):
+                    gate_weights(0, j)
+                normalise(1, 1)
+        normalise(1, T - 1)
+        on_scalar("c", 0, 1)
+        quantise_piece("c", 0, 0)
+        for j in range(J):
+            gate_messages(0, j)
+            if j == PACK:
+                regroup_gated(0, 0, False)
+            if j == PACK + 2:
+                quantise_gated(0, 0)
+        regroup_gated(0, 1, False)
+        for j in range(J):
+            gate_weights(1, j)
+        on_scalar("c", 1, 0)
+        on_scalar("c", 1, 1)
+        quantise_piece("c", 0, 1)
+        quantise_gated(0, 1)
+        for j in range(J):
+            gate_messages(1, j)
+            if j == PACK:
+                regroup_gated(1, 0, False)
+            if j == PACK + 2:
+                quantise_gated(1, 0)
+        quantise_piece("c", 1, 0)
+        regroup_gated(1, 1, False)
+        quantise_piece("c", 1, 1)
+        sum_directions(0, 0)
+        sum_directions(1, 0)
+        sum_directions(0, 1)
+        quantise_gated(1, 1)
+        sum_directions(1, 1)
+        edge_plus_b(0)
+        edge_plus_b(1)
+        for a in range(A):
+            add_bias(a)
+            out_mean(a)
+        out_var(0)
+        centre_times_gain(0)
+        out_var(1)
+        out_rstd(0)
+        centre_times_gain(1)
+        out_rstd(1)
+        for a in range(A):
+            for h in range(HALVES):
+                add_edge(a, h)
+                sigmoid(a, h)
+        for a in range(A):
+            for h in range(HALVES):
+                finish(a, h)

@@ -70,9 +70,9 @@ def tile_comformerconvedgelayer_pb_kernel(
         edge_raw = keep.tile([P, A, C], BF16)
         x_codes = {}
         x_scales = {}
-        for name, row_tiles in (("e", A), ("k", A * T), ("m", A * T)):
-            x_codes[name] = keep.tile([P, row_tiles, PASSES * P], U32, name="codes_" + name, align_bytes=64)
-            x_scales[name] = keep.tile([P, row_tiles, PASSES * P], U8, name="scales_" + name, align_bytes=64)
+        for name, groups, rows in (("e", 1, A * P), ("k", A, T * P), ("m", A, T * P)):
+            x_codes[name] = keep.tile([P, groups, PASSES, rows], U32, name="codes_" + name, align_bytes=64)
+            x_scales[name] = keep.tile([P, groups, PASSES, rows], U8, name="scales_" + name, align_bytes=64)
         g_codes = keep.tile([P, A, PASSES, T * P], U32, align_bytes=64)
         g_scales = keep.tile([P, A, PASSES, T * P], U8, align_bytes=64)
         w_codes = {}
@@ -140,19 +140,27 @@ def tile_comformerconvedgelayer_pb_kernel(
             wordsT = psum.tile([P, PASSES * 2, P], F32, tag="bank", name="wordsT")
             for s in range(PASSES * 2):
                 nc.tensor.transpose(wordsT[:, s, :], words[:, block(s)], ident_f32[:])
-            grouped[name, rt] = keep.tile(
-                [P, PASSES, P, PACK], BF16, tag="x_grouped", bufs=4, name="x_grouped", align_bytes=64
-            )
+            n = A if name == "e" else T
+            a, t = divmod(rt, n)
+            if t == 0:
+                grouped[name, a] = keep.tile(
+                    [P, PASSES, n * P, PACK], BF16, tag="x_grouped", bufs=2, name="x_grouped", align_bytes=64
+                )
             nc.scalar.copy(
-                out=grouped[name, rt][:].bitcast(F32), in_=wordsT[:].rearrange("p (g u) r -> p g r u", u=2)
+                out=grouped[name, a][:].bitcast(F32)[:, :, block(t), :],
+                in_=wordsT[:].rearrange("p (g u) r -> p g r u", u=2),
             )
 
-        def quantise_rows(name, rt):
-            nc.vector.quantize_mx(
-                out=x_codes[name][:, rt, :].bitcast(FP8X4),
-                scales=x_scales[name][:, rt, :],
-                in_=grouped[name, rt][:].rearrange("p g r f -> p (g r f)"),
-            )
+        def quantise_rows(name, a):
+            n = A * P if name == "e" else T * P
+            for g in range(PASSES):
+                for lo, hi in ((0, 2 * P), (2 * P, n)):
+                    if lo < hi:
+                        nc.vector.quantize_mx(
+                            out=x_codes[name][:, a, g, lo:hi].bitcast(FP8X4),
+                            scales=x_scales[name][:, a, g, lo:hi],
+                            in_=grouped[name, a][:, g, lo:hi, :].rearrange("p r f -> p (r f)"),
+                        )
 
         def direction_to_words(name, a, t):
             rows_to_words(name, a * T + t, raw[name + "x", a][:, t, :].bitcast(F32))
@@ -182,7 +190,7 @@ def tile_comformerconvedgelayer_pb_kernel(
             nc.scalar.copy(out=dst, in_=src)
 
         def go():
-            token = keep.tile([P, 1], F32, tag="token", bufs=4, name="token")
+            token = keep.tile([P, 1], F32, tag="token", bufs=2, name="token")
             nc.vector.memset(token[:], 1.0)
             return token
 
@@ -215,17 +223,20 @@ def tile_comformerconvedgelayer_pb_kernel(
                 in_=grouped[name, g, h][:].rearrange("p w f -> p (w f)"),
             )
 
-        def mx_group(out_cols, w, j, x, rt):
-            for g in range(PASSES):
-                nc.tensor.matmul_mx(
-                    out=out_cols,
-                    lhsT=w_codes[w][:, g, block(j)].bitcast(FP8X4),
-                    lhsT_scale=w_scales[w][:, g, block(j)],
-                    rhs=x_codes[x][:, rt, block(g)].bitcast(FP8X4),
-                    rhs_scale=x_scales[x][:, rt, block(g)],
-                    start=(g == 0),
-                    stop=(g == PASSES - 1),
-                )
+        def mx_group(out, w, j, x, a):
+            n = A * P if x == "e" else T * P
+            for lo, hi in ((0, 2 * P), (2 * P, n)):
+                if lo < hi:
+                    for g in range(PASSES):
+                        nc.tensor.matmul_mx(
+                            out=out[:, lo:hi],
+                            lhsT=w_codes[w][:, g, block(j)].bitcast(FP8X4),
+                            lhsT_scale=w_scales[w][:, g, block(j)],
+                            rhs=x_codes[x][:, a, g, lo:hi].bitcast(FP8X4),
+                            rhs_scale=x_scales[x][:, a, g, lo:hi],
+                            start=(g == 0),
+                            stop=(g == PASSES - 1),
+                        )
 
         def inverse_std(key, eps):
             var_eps = keep.tile([P, 1], F32, tag="var_eps", bufs=4, name="var_eps")
@@ -237,8 +248,7 @@ def tile_comformerconvedgelayer_pb_kernel(
 
         def query_products(j):
             acc["q", j] = bank("qT")
-            for a in range(A):
-                mx_group(acc["q", j][:, block(a)], "q", j, "e", a)
+            mx_group(acc["q", j], "q", j, "e", 0)
 
         def add_query_bias(j):
             nc.scalar.activation(
@@ -247,8 +257,7 @@ def tile_comformerconvedgelayer_pb_kernel(
 
         def key_products(a, j):
             acc["k", a, j] = bank("kT")
-            for t in range(T):
-                mx_group(acc["k", a, j][:, block(t)], "k", j, "k", a * T + t)
+            mx_group(acc["k", a, j], "k", j, "k", a)
 
         def times_query(a, j):
             nc.vector.scalar_tensor_tensor(
@@ -260,8 +269,13 @@ def tile_comformerconvedgelayer_pb_kernel(
                 op1=ALU.mult,
             )
 
-        def transpose_alpha(a, t):
+        def keep_clock(out, n):
+            nc.tensor.matmul(out=out[:, 0:n], lhsT=ident_bf[:], rhs=edge_raw[:, 0, 0:n], start=True, stop=True)
+
+        def transpose_alpha(a, t, warm=0):
             acc["alpha", a, t] = [bank("alpha%d" % h) for h in range(HALVES)]
+            for h in range(warm):
+                keep_clock(acc["alpha", a, t][h], BANK)
             for j in range(J):
                 nc.tensor.transpose(
                     acc["alpha", a, t][j // PACK][:, block(j % PACK)], alphaT[a][:, j, t, :], ident_f32[:]
@@ -290,8 +304,10 @@ def tile_comformerconvedgelayer_pb_kernel(
                     scale=rstd[a, t][:], bias=shift[a, t][:],
                 )
 
-        def gate_weights(a, j):
+        def gate_weights(a, j, warm=0):
             yT = bank("yT")
+            if warm:
+                keep_clock(yT, BANK)
             for t in range(T):
                 nc.tensor.transpose(yT[:, block(t)], ys[a, t][:, block(j)], ident_f32[:])
             nc.scalar.activation(
@@ -301,8 +317,7 @@ def tile_comformerconvedgelayer_pb_kernel(
 
         def gate_messages(a, j):
             msgT = bank("msgT")
-            for t in range(T):
-                mx_group(msgT[:, block(t)], "m", j, "m", a * T + t)
+            mx_group(msgT, "m", j, "m", a)
             nc.vector.scalar_tensor_tensor(
                 out=gated[a][:, j, :, :].rearrange("p t e -> p (t e)"),
                 in0=msgT[:, 0 : T * P],
@@ -334,7 +349,6 @@ def tile_comformerconvedgelayer_pb_kernel(
         ub = {}
         v = {}
         log = {}
-        squares = keep.tile([P, BANK], F32)
         sums = {}
         neg_mean = {}
         neg_mean_root = {}
@@ -387,6 +401,7 @@ def tile_comformerconvedgelayer_pb_kernel(
 
         def out_var(a):
             var[a] = keep.tile([P, HALVES], F32, name="var%d" % a)
+            squares = keep.tile([P, BANK], F32, tag="y", bufs=4, name="squares")
             for h in range(HALVES):
                 nc.scalar.activation(
                     out=squares[:], in_=ub[a][:, half(h)], func=ACT.Square,
@@ -408,87 +423,88 @@ def tile_comformerconvedgelayer_pb_kernel(
                     op0=ALU.add, op1=ALU.mult,
                 )
 
-        def add_edge(a, h):
+        def add_edge(a, lo, hi):
+            eb = acc["edge_b", a][lo // BANK][:, lo % BANK : (hi - 1) % BANK + 1]
             nc.vector.scalar_tensor_tensor(
-                out=v[a][:, half(h)], in0=v[a][:, half(h)], scalar=rstd["out", a][:], in1=acc["edge_b", a][h][:],
-                op0=ALU.mult, op1=ALU.add,
+                out=v[a][:, lo:hi], in0=v[a][:, lo:hi], scalar=rstd["out", a][:], in1=eb, op0=ALU.mult, op1=ALU.add
             )
 
-        def sigmoid(a, h):
-            nc.scalar.activation(out=log[a][:, half(h)], in_=v[a][:, half(h)], func=ACT.Sigmoid, scale=-1.0)
+        def sigmoid(a, lo, hi):
+            nc.scalar.activation(out=log[a][:, lo:hi], in_=v[a][:, lo:hi], func=ACT.Sigmoid, scale=-1.0)
 
-        def finish(a, h):
-            nc.scalar.activation(out=log[a][:, half(h)], in_=log[a][:, half(h)], func=ACT.Ln, bias=tiny[:])
+        def finish(a, lo, hi):
+            nc.scalar.activation(out=log[a][:, lo:hi], in_=log[a][:, lo:hi], func=ACT.Ln, bias=tiny[:])
             nc.vector.scalar_tensor_tensor(
-                out=log[a][:, half(h)], in0=log[a][:, half(h)], scalar=-1.0, in1=v[a][:, half(h)],
+                out=log[a][:, lo:hi], in0=log[a][:, lo:hi], scalar=-1.0, in1=v[a][:, lo:hi],
                 op0=ALU.mult, op1=ALU.max,
             )
-            nc.sync.dma_start(out=out[a * P : (a + 1) * P, half(h)], in_=log[a][:, half(h)])
+            nc.sync.dma_start(out=out[a * P : (a + 1) * P, lo:hi], in_=log[a][:, lo:hi])
 
 
         load_columns()
         warm_up()
-        load_edge()
         load_w("q", 0)
+        load_edge()
         load_w("q", 1)
-        load_x("k", 0)
         load_w("k", 0)
+        load_x("k", 0)
         load_w("k", 1)
         load_x("k", 1)
         load_x("m", 0)
-        load_x("m", 1)
         load_w("m", 0)
         load_w("m", 1)
+        load_x("m", 1)
         load_w("c", 0)
         load_w("c", 1)
         load_vectors()
 
-        for a in range(A):
-            rows_to_words("e", a, edge_raw[:, a, :].bitcast(F32))
-        vec_cols = psum.tile([P, P], BF16, tag="bank", name="vec_cols")
-        nc.tensor.transpose(vec_cols[:], vec_rows[:], ident_bf[:])
-        nc.vector.tensor_copy(out=chan[:], in_=vec_cols[:, 0 : 5 * J])
-        for a in range(A):
-            quantise_rows("e", a)
         new_weight("q")
         on_vector("q", 0, 0)
         on_scalar("q", 0, 1)
-        on_vector("q", 1, 0)
-        on_scalar("q", 1, 1)
+        for a in range(A):
+            rows_to_words("e", a, edge_raw[:, a, :].bitcast(F32))
         quantise_piece("q", 0, 0)
         quantise_piece("q", 0, 1)
+        on_vector("q", 1, 0)
+        quantise_rows("e", 0)
+        on_scalar("q", 1, 1)
         quantise_piece("q", 1, 0)
-        quantise_piece("q", 1, 1)
-        for t in range(T):
-            direction_to_words("k", 0, t)
-        for j in range(J):
-            query_products(j)
+        vec_cols = psum.tile([P, P], BF16, tag="bank", name="vec_cols")
+        nc.tensor.transpose(vec_cols[:], vec_rows[:], ident_bf[:])
+        nc.vector.tensor_copy(out=chan[:], in_=vec_cols[:, 0 : 5 * J])
         new_weight("k")
         on_vector("k", 0, 0)
+        quantise_piece("q", 1, 1)
         on_scalar("k", 0, 1)
+        for j in range(4):
+            query_products(j)
+        quantise_piece("k", 0, 0)
         for t in range(T):
-            quantise_rows("k", t)
+            direction_to_words("k", 0, t)
+        for j in range(4, J):
+            query_products(j)
         for j in range(J):
             add_query_bias(j)
-        on_vector("k", 1, 0)
-        quantise_piece("k", 0, 0)
-        on_vector("k", 1, 1)
         quantise_piece("k", 0, 1)
+        on_vector("k", 1, 0)
+        quantise_rows("k", 0)
+        on_vector("k", 1, 1)
         quantise_piece("k", 1, 0)
         for t in range(T):
             direction_to_words("k", 1, t)
-        for t in range(T):
-            direction_to_words("m", 0, t)
         for j in range(J // 2):
             key_products(0, j)
         quantise_piece("k", 1, 1)
+        quantise_rows("k", 1)
         for t in range(T):
-            quantise_rows("k", T + t)
+            direction_to_words("m", 0, t)
         for j in range(J // 2, J):
             key_products(0, j)
         new_weight("m")
-        on_scalar("m", 0, 0)
+        half_on_gpsimd("m", 0, 0, 0, True)
+        half_on_gpsimd("m", 0, 0, 1, False)
         on_scalar("m", 1, 0)
+        on_scalar("m", 0, 1)
         for j in range(J):
             times_query(0, j)
         for j in range(2):
@@ -501,8 +517,7 @@ def tile_comformerconvedgelayer_pb_kernel(
                 times_query(1, j)
             row_stats(0, t)
             if t == 0:
-                for tt in range(T):
-                    quantise_rows("m", tt)
+                quantise_rows("m", 0)
             else:
                 quantise_piece("m", t - 1, 0)
             row_scale(0, t)
@@ -511,42 +526,42 @@ def tile_comformerconvedgelayer_pb_kernel(
             if t == 0:
                 for tt in range(T):
                     direction_to_words("m", 1, tt)
-            if t == 1:
-                on_scalar("m", 0, 1)
             normalise(0, t)
+            if t == 1:
+                on_scalar("c", 0, 1)
         for j in (J - 2, J - 1):
             times_query(1, j)
         for t in range(2):
             transpose_alpha(1, t)
-        for t in range(T):
-            quantise_rows("m", T + t)
+        quantise_rows("m", 1)
         new_weight("c")
-        for t in range(T):
-            row_stats(1, t)
-            if t < 2:
-                quantise_piece("m", t, 1)
-            else:
-                on_vector("c", 0, 0)
-            row_scale(1, t)
-            if t == 0:
-                for j in range(4):
-                    gate_weights(0, j)
-                transpose_alpha(1, 2)
-            if t == 1:
-                normalise(1, 0)
-                for j in range(4, J):
-                    gate_weights(0, j)
-                normalise(1, 1)
-        normalise(1, T - 1)
-        on_scalar("c", 0, 1)
-        quantise_piece("c", 0, 0)
-        for j in range(J):
+        half_on_gpsimd("c", 0, 0, 0, True)
+        row_stats(1, 0)
+        quantise_piece("m", 0, 1)
+        row_scale(1, 0)
+        for j in range(4):
+            gate_weights(0, j)
+        quantise_piece("m", 1, 1)
+        row_stats(1, 1)
+        half_on_gpsimd("c", 0, 0, 1, False)
+        normalise(1, 0)
+        for j in range(2):
             gate_messages(0, j)
-            if j == PACK:
-                regroup_gated(0, 0, False)
-            if j == PACK + 2:
-                quantise_gated(0, 0)
+        transpose_alpha(1, 2)
+        row_scale(1, 1)
+        for j in range(4, J):
+            gate_weights(0, j)
+        row_stats(1, 2)
+        normalise(1, 1)
+        row_scale(1, 2)
+        normalise(1, 2)
+        for j in range(2, J):
+            gate_messages(0, j)
+            if j == PACK - 1:
+                regroup_gated(0, 0, True)
+        quantise_piece("c", 0, 0)
         regroup_gated(0, 1, False)
+        quantise_gated(0, 0)
         for j in range(J):
             gate_weights(1, j)
         on_scalar("c", 1, 0)
@@ -578,10 +593,8 @@ def tile_comformerconvedgelayer_pb_kernel(
         out_rstd(0)
         centre_times_gain(1)
         out_rstd(1)
-        for a in range(A):
-            for h in range(HALVES):
-                add_edge(a, h)
-                sigmoid(a, h)
-        for a in range(A):
-            for h in range(HALVES):
-                finish(a, h)
+        for a, lo, hi in ((0, 0, 512), (0, 512, 1024), (1, 0, 512), (1, 512, 1024)):
+            add_edge(a, lo, hi)
+            sigmoid(a, lo, hi)
+        for a, lo, hi in ((0, 0, 512), (0, 512, 1024), (1, 0, 512), (1, 512, 1024)):
+            finish(a, lo, hi)

import concourse.mybir as mybir
from concourse.masks import make_identity

F32 = mybir.dt.float32
BF16 = mybir.dt.bfloat16
U32 = mybir.dt.uint32
U8 = mybir.dt.uint8
FP8X4 = mybir.dt.float8_e4m3fn_x4
ALU = mybir.AluOpType
ACT = mybir.ActivationFunctionType

P = 128
E = 256
T = 3
C = 1024
A = E // P
J = C // P
PACK = 4
K_PASS = P * PACK
PASSES = C // K_PASS
BANK = 512
HALVES = C // BANK
EPS = 1e-5
TINY = 2.0 ** -60

FLOPS = 2 * C * C * (E + 3 * E * T)

BQ, BK, BM, GA, BA = 0, J, 2 * J, 3 * J, 4 * J


def half(h):
    return slice(h * BANK, (h + 1) * BANK)


def block(i):
    return slice(i * P, (i + 1) * P)


def tile_comformerconvedgelayer_pb_kernel(
    tc, edge, h_k, h_m, Wq, bq, Wk2, bk2, Wm2, bm2, Wc, bc, g_att, b_att, g_bn, b_bn, out
):
    nc = tc.nc
    with tc.tile_pool(name="keep", bufs=1) as keep, tc.psum_pool(name="psum", bufs=8) as psum, tc.manual_schedule():

        def bank(name):
            return psum.tile([P, BANK], F32, tag="bank", name=name)

        ident_f32 = keep.tile([P, P], F32)
        make_identity(nc, ident_f32[:])
        ident_bf = keep.tile([P, P], BF16)
        make_identity(nc, ident_bf[:])
        neg_half = keep.tile([P, 1], F32)
        nc.vector.memset(neg_half[:], -0.5)
        tiny = keep.tile([P, 1], F32)
        nc.vector.memset(tiny[:], TINY)
        vec_rows = keep.tile([P, P], BF16)
        nc.vector.memset(vec_rows[:], 0.0)
        chan = keep.tile([P, 5 * J], F32)
        b_row = keep.tile([P, C], BF16)
        nc.vector.memset(b_row[:], 0.0)
        warm = keep.tile([P, 1], F32)

        def warm_up():
            nc.scalar.activation(out=warm[:], in_=neg_half[:], func=ACT.Sigmoid)


        def chan_col(base, j):
            return chan[:, base + j : base + j + 1]

        edge_raw = keep.tile([P, A, C], BF16)
        x_codes = {}
        x_scales = {}
        for name, groups, rows in (("e", 1, A * P), ("k", A, T * P), ("m", A, T * P)):
            x_codes[name] = keep.tile([P, groups, PASSES, rows], U32, name="codes_" + name, align_bytes=64)
            x_scales[name] = keep.tile([P, groups, PASSES, rows], U8, name="scales_" + name, align_bytes=64)
        g_codes = keep.tile([P, A, PASSES, T * P], U32, align_bytes=64)
        g_scales = keep.tile([P, A, PASSES, T * P], U8, align_bytes=64)
        w_codes = {}
        w_scales = {}
        qbT = keep.tile([P, J, E], F32)
        alphaT = [keep.tile([P, J, T, P], F32, tag="alphaT", bufs=2, name="alphaT") for a in range(A)]
        sigT = [keep.tile([P, J, T * P], F32, name="sigT%d" % a) for a in range(A)]
        gated = [keep.tile([P, J, T, P], BF16, name="gated%d" % a) for a in range(A)]
        bc_all = keep.tile([P, C], BF16)
        g_all = keep.tile([P, C], BF16)
        acc = {}
        raw = {}
        grouped = {}
        stats = {}
        rstd = {}
        shift = {}
        mean_var = {}
        ys = {}

        def load_rows(name, x, a):
            raw[name, a] = keep.tile([P, T, C], BF16, tag="rows_raw", bufs=3, name="rows_raw")
            nc.sync.dma_start(out=raw[name, a][:], in_=x[a * P : (a + 1) * P, :, :])

        def new_raw(name, g):
            raw[name, g] = keep.tile([P, PACK, C], BF16, tag="w_raw", bufs=4, name="w_raw")

        def load_pairs(name, w, g):
            new_raw(name, g)
            nc.sync.dma_start(
                out=raw[name, g][:].rearrange("p (u e) w -> p u (e w)", u=2),
                in_=w[g * K_PASS : (g + 1) * K_PASS, :].rearrange("(u p e) w -> p u (e w)", u=2, p=P),
            )

        def load_rows_of_128(name, w, g):
            new_raw(name, g)
            nc.sync.dma_start(
                out=raw[name, g][:], in_=w[g * K_PASS : (g + 1) * K_PASS, :].rearrange("(f p) w -> p f w", p=P)
            )

        def raw_columns(name, g, lo, hi):
            return raw[name, g][:, :, lo:hi]

        def load_edge():
            nc.sync.dma_start(out=edge_raw[:], in_=edge.rearrange("(a p) c -> p a c", p=P))

        def load_x(name, a):
            load_rows(name + "x", h_k if name == "k" else h_m, a)

        def load_w(name, g):
            if name == "c":
                load_rows_of_128(name, Wc, g)
            else:
                load_pairs(name, {"q": Wq, "k": Wk2, "m": Wm2}[name], g)

        def load_columns():
            for i, vec in enumerate((bq, bk2, bm2, g_att, b_att)):
                nc.scalar.dma_start(out=vec_rows[i * J : (i + 1) * J, :], in_=vec.rearrange("(j p) -> j p", p=P))

        def load_vectors():
            nc.sync.dma_start(out=b_row[0:1, :], in_=b_bn.rearrange("(o c) -> o c", o=1))
            nc.sync.dma_start(out=bc_all[:], in_=bc.partition_broadcast(P))
            nc.sync.dma_start(out=g_all[:], in_=g_bn.partition_broadcast(P))

        def rows_to_words(name, rt, words):
            wordsT = psum.tile([P, PASSES * 2, P], F32, tag="bank", name="wordsT")
            for s in range(PASSES * 2):
                nc.tensor.transpose(wordsT[:, s, :], words[:, block(s)], ident_f32[:])
            n = A if name == "e" else T
            a, t = divmod(rt, n)
            if t == 0:
                grouped[name, a] = keep.tile(
                    [P, PASSES, n * P, PACK], BF16, tag="x_grouped", bufs=2, name="x_grouped", align_bytes=64
                )
            nc.scalar.copy(
                out=grouped[name, a][:].bitcast(F32)[:, :, block(t), :],
                in_=wordsT[:].rearrange("p (g u) r -> p g r u", u=2),
            )

        def quantise_rows(name, a):
            n = A * P if name == "e" else T * P
            for g in range(PASSES):
                for lo, hi in ((0, 2 * P), (2 * P, n)):
                    if lo < hi:
                        nc.vector.quantize_mx(
                            out=x_codes[name][:, a, g, lo:hi].bitcast(FP8X4),
                            scales=x_scales[name][:, a, g, lo:hi],
                            in_=grouped[name, a][:, g, lo:hi, :].rearrange("p r f -> p (r f)"),
                        )

        def direction_to_words(name, a, t):
            rows_to_words(name, a * T + t, raw[name + "x", a][:, t, :].bitcast(F32))

        def new_weight(name):
            w_codes[name] = keep.tile([P, PASSES, C], U32, tag="w_codes", bufs=3, name="w_codes", align_bytes=64)
            w_scales[name] = keep.tile([P, PASSES, C], U8, tag="w_scales", bufs=3, name="w_scales", align_bytes=64)

        def new_grouped(name, g, h):
            grouped[name, g, h] = keep.tile(
                [P, BANK, PACK], BF16, tag="w_grouped", bufs=5, name="w_grouped", align_bytes=64
            )

        def four_columns(name, g, h, lo, hi):
            dst = grouped[name, g, h][:, lo:hi, :].rearrange("p (c i) f -> p c f i", i=4)
            src = raw_columns(name, g, h * BANK + lo, h * BANK + hi).rearrange("p f (c i) -> p c f i", i=4)
            return dst, src

        def on_vector(name, g, h):
            new_grouped(name, g, h)
            dst, src = four_columns(name, g, h, 0, BANK)
            nc.vector.tensor_copy(out=dst, in_=src)

        def on_scalar(name, g, h):
            new_grouped(name, g, h)
            dst, src = four_columns(name, g, h, 0, BANK)
            nc.scalar.copy(out=dst, in_=src)

        def go():
            token = keep.tile([P, 1], F32, tag="token", bufs=2, name="token")
            nc.vector.memset(token[:], 1.0)
            return token

        def half_on_gpsimd(name, g, h, part, wait):
            if part == 0:
                new_grouped(name, g, h)
            lo = part * BANK // 2
            nc.gpsimd.tensor_scalar(
                out=grouped[name, g, h][:, lo : lo + BANK // 2, :],
                in0=raw_columns(name, g, h * BANK + lo, h * BANK + lo + BANK // 2).rearrange("p f w -> p w f"),
                scalar1=go()[:] if wait else 1.0, scalar2=0.0, op0=ALU.mult, op1=ALU.add,
            )

        def on_tensor(name, g, h):
            new_grouped(name, g, h)
            for lo in (0, BANK // 2):
                words = psum.tile([P, BANK // 2, PACK], BF16, tag="bank", name="words")
                for c in range(2):
                    first = h * BANK + lo + c * P
                    nc.tensor.matmul(
                        out=words[:, block(c), :], lhsT=ident_bf[:],
                        rhs=raw_columns(name, g, first, first + P).rearrange("p f n -> p n f"), start=True, stop=True,
                    )
                nc.scalar.copy(out=grouped[name, g, h][:, lo : lo + BANK // 2, :], in_=words[:])

        def quantise_piece(name, g, h):
            nc.vector.quantize_mx(
                out=w_codes[name][:, g, half(h)].bitcast(FP8X4),
                scales=w_scales[name][:, g, half(h)],
                in_=grouped[name, g, h][:].rearrange("p w f -> p (w f)"),
            )

        def mx_group(out, w, j, x, a):
            n = A * P if x == "e" else T * P
            for lo, hi in ((0, 2 * P), (2 * P, n)):
                if lo < hi:
                    for g in range(PASSES):
                        nc.tensor.matmul_mx(
                            out=out[:, lo:hi],
                            lhsT=w_codes[w][:, g, block(j)].bitcast(FP8X4),
                            lhsT_scale=w_scales[w][:, g, block(j)],
                            rhs=x_codes[x][:, a, g, lo:hi].bitcast(FP8X4),
                            rhs_scale=x_scales[x][:, a, g, lo:hi],
                            start=(g == 0),
                            stop=(g == PASSES - 1),
                        )

        def inverse_std(key, eps):
            var_eps = keep.tile([P, 1], F32, tag="var_eps", bufs=4, name="var_eps")
            nc.gpsimd.tensor_scalar(
                out=var_eps[:], in0=mean_var[key][:, 1:2], scalar1=eps, scalar2=1.0, op0=ALU.add, op1=ALU.mult
            )
            rstd[key] = keep.tile([P, 1], F32, tag="rstd", bufs=4, name="rstd")
            nc.gpsimd.tensor_tensor(out=rstd[key][:], in0=var_eps[:], in1=neg_half[:], op=ALU.pow)

        def query_products(j):
            acc["q", j] = bank("qT")
            mx_group(acc["q", j], "q", j, "e", 0)

        def add_query_bias(j):
            nc.scalar.activation(
                out=qbT[:, j, :], in_=acc["q", j][:, 0:E], func=ACT.Identity, bias=chan_col(BQ, j), scale=1.0
            )

        def key_products(a, j):
            acc["k", a, j] = bank("kT")
            mx_group(acc["k", a, j], "k", j, "k", a)

        def times_query(a, j):
            nc.vector.scalar_tensor_tensor(
                out=alphaT[a][:, j, :, :],
                in0=acc["k", a, j][:, 0 : T * P].rearrange("p (t e) -> p t e", t=T),
                scalar=chan_col(BK, j),
                in1=qbT[:, j, block(a)].unsqueeze(1).to_broadcast([P, T, P]),
                op0=ALU.add,
                op1=ALU.mult,
            )

        def keep_clock(out, n):
            nc.tensor.matmul(out=out[:, 0:n], lhsT=ident_bf[:], rhs=edge_raw[:, 0, 0:n], start=True, stop=True)

        def transpose_alpha(a, t, warm=0):
            acc["alpha", a, t] = [bank("alpha%d" % h) for h in range(HALVES)]
            for h in range(warm):
                keep_clock(acc["alpha", a, t][h], BANK)
            for j in range(J):
                nc.tensor.transpose(
                    acc["alpha", a, t][j // PACK][:, block(j % PACK)], alphaT[a][:, j, t, :], ident_f32[:]
                )

        def row_stats(a, t):
            stats[a, t] = keep.tile([P, HALVES, 6], F32, tag="stats", bufs=4, name="stats")
            for h in range(HALVES):
                nc.vector.bn_stats(out=stats[a, t][:, h, :], in_=acc["alpha", a, t][h][:])

        def row_scale(a, t):
            mean_var[a, t] = keep.tile([P, 2], F32, tag="mean_var", bufs=4, name="mean_var")
            nc.vector.bn_aggr(out=mean_var[a, t][:], in_=stats[a, t][:].rearrange("p h s -> p (h s)"))
            inverse_std((a, t), C * EPS)
            shift[a, t] = keep.tile([P, 1], F32, tag="shift", bufs=4, name="shift")
            nc.gpsimd.tensor_scalar(
                out=shift[a, t][:], in0=mean_var[a, t][:, 0:1], scalar1=rstd[a, t][:], scalar2=-1.0,
                op0=ALU.mult, op1=ALU.mult,
            )

        def normalise(a, t):
            ys[a, t] = keep.tile([P, C], F32, tag="y", bufs=4, name="y")
            for h in range(HALVES):
                nc.scalar.activation(
                    out=ys[a, t][:, half(h)], in_=acc["alpha", a, t][h][:], func=ACT.Identity,
                    scale=rstd[a, t][:], bias=shift[a, t][:],
                )

        def gate_weights(a, j, warm=0):
            yT = bank("yT")
            if warm:
                keep_clock(yT, BANK)
            for t in range(T):
                nc.tensor.transpose(yT[:, block(t)], ys[a, t][:, block(j)], ident_f32[:])
            nc.scalar.activation(
                out=sigT[a][:, j, :], in_=yT[:, 0 : T * P], func=ACT.Sigmoid,
                scale=chan_col(GA, j), bias=chan_col(BA, j),
            )

        def gate_messages(a, j):
            msgT = bank("msgT")
            mx_group(msgT, "m", j, "m", a)
            nc.vector.scalar_tensor_tensor(
                out=gated[a][:, j, :, :].rearrange("p t e -> p (t e)"),
                in0=msgT[:, 0 : T * P],
                scalar=chan_col(BM, j),
                in1=sigT[a][:, j, :],
                op0=ALU.add,
                op1=ALU.mult,
            )

        def regroup_gated(a, g, gpsimd):
            grouped["g", a, g] = keep.tile(
                [P, T * P, PACK], BF16, tag="gated_grouped", bufs=2, name="gated_grouped", align_bytes=64
            )
            dst = grouped["g", a, g][:]
            src = gated[a][:, g * PACK : (g + 1) * PACK, :, :].rearrange("p f t e -> p (t e) f")
            if gpsimd:
                nc.gpsimd.tensor_scalar(out=dst, in0=src, scalar1=1.0, scalar2=0.0, op0=ALU.mult, op1=ALU.add)
            else:
                nc.vector.tensor_copy(out=dst, in_=src)

        def quantise_gated(a, g):
            for lo, hi in ((0, 2 * P), (2 * P, 3 * P)):
                nc.vector.quantize_mx(
                    out=g_codes[:, a, g, lo:hi].bitcast(FP8X4),
                    scales=g_scales[:, a, g, lo:hi],
                    in_=grouped["g", a, g][:, lo:hi, :].rearrange("p r f -> p (r f)"),
                )

        ub = {}
        v = {}
        log = {}
        sums = {}
        neg_mean = {}
        neg_mean_root = {}
        var = {}

        def sum_directions(a, g):
            if g == 0:
                acc["u", a] = [bank("u%d" % h) for h in range(HALVES)]
            for h in range(HALVES):
                for t in range(T):
                    nc.tensor.matmul_mx(
                        out=acc["u", a][h][:],
                        lhsT=g_codes[:, a, g, block(t)].bitcast(FP8X4),
                        lhsT_scale=g_scales[:, a, g, block(t)],
                        rhs=w_codes["c"][:, g, half(h)].bitcast(FP8X4),
                        rhs_scale=w_scales["c"][:, g, half(h)],
                        start=(g == 0 and t == 0),
                        stop=(g == PASSES - 1 and t == T - 1),
                    )

        def edge_plus_b(a):
            acc["edge_b", a] = [bank("edge_b%d" % h) for h in range(HALVES)]
            for h in range(HALVES):
                nc.tensor.matmul(
                    out=acc["edge_b", a][h][:], lhsT=ident_bf[:], rhs=edge_raw[:, a, half(h)], start=True, stop=False
                )
                nc.tensor.matmul(
                    out=acc["edge_b", a][h][:], lhsT=ident_bf[:, 0:1].to_broadcast([P, P]), rhs=b_row[:, half(h)],
                    start=False, stop=True,
                )

        def add_bias(a):
            late = keep.tile([P, 3, C], F32, tag="alphaT", bufs=2, name="late")
            ub[a], v[a], log[a] = [late[:, i, :] for i in range(3)]
            sums[a] = keep.tile([P, HALVES], F32, name="sums%d" % a)
            for h in range(HALVES):
                nc.vector.scalar_tensor_tensor(
                    out=ub[a][:, half(h)], in0=bc_all[:, half(h)], scalar=float(T), in1=acc["u", a][h][:],
                    op0=ALU.mult, op1=ALU.add, accum_out=sums[a][:, h : h + 1],
                )

        def out_mean(a):
            neg_mean[a] = keep.tile([P, 1], F32, name="neg_mean%d" % a)
            neg_mean_root[a] = keep.tile([P, 1], F32, name="neg_mean_root%d" % a)
            for dst, factor in ((neg_mean_root[a], -1.0 / (C * C ** 0.5)), (neg_mean[a], -1.0 / C)):
                nc.gpsimd.tensor_scalar(
                    out=dst[:], in0=sums[a][:, 0:1], scalar1=sums[a][:, 1:2], scalar2=factor,
                    op0=ALU.add, op1=ALU.mult,
                )

        def out_var(a):
            var[a] = keep.tile([P, HALVES], F32, name="var%d" % a)
            squares = keep.tile([P, BANK], F32, tag="y", bufs=4, name="squares")
            for h in range(HALVES):
                nc.scalar.activation(
                    out=squares[:], in_=ub[a][:, half(h)], func=ACT.Square,
                    scale=C ** -0.5, bias=neg_mean_root[a][:], accum_out=var[a][:, h : h + 1],
                )

        def out_rstd(a):
            var_eps = keep.tile([P, 1], F32, name="out_var_eps%d" % a)
            nc.gpsimd.tensor_scalar(
                out=var_eps[:], in0=var[a][:, 0:1], scalar1=var[a][:, 1:2], scalar2=EPS, op0=ALU.add, op1=ALU.add
            )
            rstd["out", a] = keep.tile([P, 1], F32, name="rstd_out%d" % a)
            nc.gpsimd.tensor_tensor(out=rstd["out", a][:], in0=var_eps[:], in1=neg_half[:], op=ALU.pow)

        def centre_times_gain(a):
            for h in range(HALVES):
                nc.vector.scalar_tensor_tensor(
                    out=v[a][:, half(h)], in0=ub[a][:, half(h)], scalar=neg_mean[a][:], in1=g_all[:, half(h)],
                    op0=ALU.add, op1=ALU.mult,
                )

        def add_edge(a, lo, hi):
            eb = acc["edge_b", a][lo // BANK][:, lo % BANK : (hi - 1) % BANK + 1]
            nc.vector.scalar_tensor_tensor(
                out=v[a][:, lo:hi], in0=v[a][:, lo:hi], scalar=rstd["out", a][:], in1=eb, op0=ALU.mult, op1=ALU.add
            )

        def sigmoid(a, lo, hi):
            nc.scalar.activation(out=log[a][:, lo:hi], in_=v[a][:, lo:hi], func=ACT.Sigmoid, scale=-1.0)

        def finish(a, lo, hi):
            nc.scalar.activation(out=log[a][:, lo:hi], in_=log[a][:, lo:hi], func=ACT.Ln, bias=tiny[:])
            nc.vector.scalar_tensor_tensor(
                out=log[a][:, lo:hi], in0=log[a][:, lo:hi], scalar=-1.0, in1=v[a][:, lo:hi],
                op0=ALU.mult, op1=ALU.max,
            )
            nc.sync.dma_start(out=out[a * P : (a + 1) * P, lo:hi], in_=log[a][:, lo:hi])


        load_columns()
        warm_up()
        load_w("q", 0)
        load_edge()
        load_w("q", 1)
        load_w("k", 0)
        load_x("k", 0)
        load_w("k", 1)
        load_x("k", 1)
        load_x("m", 0)
        load_w("m", 0)
        load_w("m", 1)
        load_x("m", 1)
        load_w("c", 0)
        load_w("c", 1)
        load_vectors()

        new_weight("q")
        on_vector("q", 0, 0)
        on_scalar("q", 0, 1)
        for a in range(A):
            rows_to_words("e", a, edge_raw[:, a, :].bitcast(F32))
        quantise_piece("q", 0, 0)
        quantise_piece("q", 0, 1)
        on_vector("q", 1, 0)
        quantise_rows("e", 0)
        on_scalar("q", 1, 1)
        quantise_piece("q", 1, 0)
        vec_cols = psum.tile([P, P], BF16, tag="bank", name="vec_cols")
        nc.tensor.transpose(vec_cols[:], vec_rows[:], ident_bf[:])
        nc.vector.tensor_copy(out=chan[:], in_=vec_cols[:, 0 : 5 * J])
        new_weight("k")
        on_vector("k", 0, 0)
        quantise_piece("q", 1, 1)
        on_scalar("k", 0, 1)
        for j in range(4):
            query_products(j)
        quantise_piece("k", 0, 0)
        for t in range(T):
            direction_to_words("k", 0, t)
        for j in range(4, J):
            query_products(j)
        for j in range(J):
            add_query_bias(j)
        quantise_piece("k", 0, 1)
        on_vector("k", 1, 0)
        quantise_rows("k", 0)
        on_vector("k", 1, 1)
        quantise_piece("k", 1, 0)
        for t in range(T):
            direction_to_words("k", 1, t)
        for j in range(J // 2):
            key_products(0, j)
        quantise_piece("k", 1, 1)
        quantise_rows("k", 1)
        for t in range(T):
            direction_to_words("m", 0, t)
        for j in range(J // 2, J):
            key_products(0, j)
        new_weight("m")
        half_on_gpsimd("m", 0, 0, 0, True)
        half_on_gpsimd("m", 0, 0, 1, False)
        on_scalar("m", 1, 0)
        on_scalar("m", 0, 1)
        for j in range(J):
            times_query(0, j)
        for j in range(2):
            key_products(1, j)
        for t in range(T):
            transpose_alpha(0, t)
            for j in (2 * t + 2, 2 * t + 3):
                key_products(1, j)
            for j in (2 * t, 2 * t + 1):
                times_query(1, j)
            row_stats(0, t)
            if t == 0:
                quantise_rows("m", 0)
            else:
                quantise_piece("m", t - 1, 0)
            row_scale(0, t)
            if t < 2:
                half_on_gpsimd("m", 1, 1, t, False)
            if t == 0:
                for tt in range(T):
                    direction_to_words("m", 1, tt)
            normalise(0, t)
            if t == 1:
                on_scalar("c", 0, 1)
        for j in (J - 2, J - 1):
            times_query(1, j)
        for t in range(2):
            transpose_alpha(1, t)
        quantise_rows("m", 1)
        new_weight("c")
        half_on_gpsimd("c", 0, 0, 0, True)
        row_stats(1, 0)
        quantise_piece("m", 0, 1)
        row_scale(1, 0)
        for j in range(4):
            gate_weights(0, j)
        quantise_piece("m", 1, 1)
        row_stats(1, 1)
        half_on_gpsimd("c", 0, 0, 1, False)
        normalise(1, 0)
        for j in range(2):
            gate_messages(0, j)
        transpose_alpha(1, 2)
        row_scale(1, 1)
        for j in range(4, J):
            gate_weights(0, j)
        row_stats(1, 2)
        normalise(1, 1)
        row_scale(1, 2)
        normalise(1, 2)
        for j in range(2, J):
            gate_messages(0, j)
            if j == PACK - 1:
                regroup_gated(0, 0, True)
        quantise_piece("c", 0, 0)
        regroup_gated(0, 1, False)
        quantise_gated(0, 0)
        for j in range(J):
            gate_weights(1, j)
        on_scalar("c", 1, 0)
        on_scalar("c", 1, 1)
        quantise_piece("c", 0, 1)
        quantise_gated(0, 1)
        for j in range(J):
            gate_messages(1, j)
            if j == PACK:
                regroup_gated(1, 0, False)
            if j == PACK + 2:
                quantise_gated(1, 0)
        quantise_piece("c", 1, 0)
        regroup_gated(1, 1, False)
        quantise_piece("c", 1, 1)
        sum_directions(0, 0)
        sum_directions(1, 0)
        sum_directions(0, 1)
        quantise_gated(1, 1)
        sum_directions(1, 1)
        edge_plus_b(0)
        edge_plus_b(1)
        for a in range(A):
            add_bias(a)
            out_mean(a)
        out_var(0)
        centre_times_gain(0)
        out_var(1)
        out_rstd(0)
        centre_times_gain(1)
        out_rstd(1)
        for a, lo, hi in ((0, 0, 512), (0, 512, 1024), (1, 0, 512), (1, 512, 1024)):
            add_edge(a, lo, hi)
            sigmoid(a, lo, hi)
        for a, lo, hi in ((0, 0, 512), (0, 512, 1024), (1, 0, 512), (1, 512, 1024)):
            finish(a, lo, hi)
